import numpy as np
import ml_dtypes


def mxq(x, axis, fmt="e4m3"):
    dtype, down = {"e4m3": (ml_dtypes.float8_e4m3fn, 7), "e5m2": (ml_dtypes.float8_e5m2, 14)}[fmt]
    v = np.moveaxis(np.asarray(x, np.float32).astype(ml_dtypes.bfloat16).astype(np.float64), axis, -1)
    blocks = v.reshape(v.shape[:-1] + (-1, 32))
    amax = np.abs(blocks).max(-1, keepdims=True)
    byte = np.maximum(np.where(amax > 0, np.frexp(amax)[1] - 1 + 127, 0) - down, 1)
    scale = np.exp2(byte - 127.0)
    codes = (blocks / scale).astype(np.float32).astype(dtype).astype(np.float64)
    return np.moveaxis((codes * scale).reshape(v.shape), -1, axis)


WIDE = False


def mx_kscale(k):
    if not WIDE:
        return np.ones(k)
    levels = np.array([10, -10, 5, -5, 0])
    a = np.random.permutation(np.resize(levels, k // 512 * 4)).reshape(k // 512, 4)
    idx = np.arange(k)
    return np.exp2(a[idx // 512, idx % 128 // 32])


BF16 = ml_dtypes.bfloat16


def bf(x):
    return np.asarray(x, np.float32).astype(BF16)


def f64(x):
    return np.asarray(x).astype(np.float64)


E2M1 = np.array([0.0, 0.5, 1.0, 1.5, 2.0, 3.0, 4.0, 6.0, -0.0, -0.5, -1.0, -1.5, -2.0, -3.0, -4.0, -6.0])


def pack_weight(w, fmt):
    k, n = w.shape
    w = f64(bf(w)).reshape(k // 32, 32, n)
    amax = np.abs(w).max(1)
    if fmt == "e4m3":
        byte = np.frexp(amax)[1] - 1 + 127 - 7
    else:
        mant, ex = np.frexp(amax / 6.0)
        byte = np.where(mant > 0.5, ex, ex - 1) + 127
    byte = np.clip(np.where(amax > 0, byte, 1), 1, 254)
    scaled = (w * np.exp2(127.0 - byte)[:, None, :]).reshape(k, n).astype(np.float32)
    by_word = np.ascontiguousarray(scaled.reshape(k // 512, 128, 4, n).transpose(0, 1, 3, 2))
    if fmt == "e4m3":
        words = by_word.astype(ml_dtypes.float8_e4m3fn).view(np.uint8)
    else:
        c = by_word.astype(ml_dtypes.float4_e2m1fn).view(np.uint8) & 0xF
        words = c[..., 0::2] | (c[..., 1::2] << 4)
    return np.ascontiguousarray(words), np.ascontiguousarray(byte.astype(np.uint8).reshape(k // 512, 16, n))


def unpack_weight(words, scales, fmt):
    g, p, n, _ = words.shape
    if fmt == "e4m3":
        vals = np.ascontiguousarray(words).view(ml_dtypes.float8_e4m3fn).astype(np.float64)
    else:
        nib = np.empty((g, p, n, 4), np.uint8)
        nib[..., 0::2] = words & 0xF
        nib[..., 1::2] = words >> 4
        vals = E2M1[nib]
    vals = vals * np.repeat(np.exp2(scales.astype(np.float64) - 127.0), 8, axis=1)[..., None]
    return vals.transpose(0, 1, 3, 2).reshape(g * 512, n)

def pack4(w):
    words, scales = pack_weight(w, "e2m1")
    return words.reshape(words.shape[0], 128, -1), scales


def unpack4(words, scales):
    return unpack_weight(words.reshape(words.shape[0], 128, -1, 2), scales, "e2m1")


B, I, H = 4096, 512, 512
G = 2 * H
EPS = 1e-5


def ln(v):
    mu = v.mean(-1, keepdims=True)
    var = np.square(v - mu).mean(-1, keepdims=True)
    return (v - mu) / np.sqrt(var + EPS)


def sigmoid(v):
    return 1.0 / (1.0 + np.exp(-v))


def setup_inputs():
    s, t = mx_kscale(I), mx_kscale(H)
    x = bf(np.random.standard_normal((B, I)) * s)
    h = bf(np.random.standard_normal((B, H)) * t)
    irz_words, irz_scales = pack4((np.random.standard_normal((G, I)) / np.sqrt(I) / s).T)
    b_irz = bf(np.random.standard_normal(G) * 0.5)
    hrz_words, hrz_scales = pack4((np.random.standard_normal((G, H)) / np.sqrt(H) / t).T)
    b_hrz = bf(np.random.standard_normal(G) * 0.5)
    return {"x": x,
            "h": h,
            "W_irz_words": irz_words,
            "W_irz_scales": irz_scales,
            "b_irz": b_irz,
            "W_hrz_words": hrz_words,
            "W_hrz_scales": hrz_scales,
            "b_hrz": b_hrz}


def reference(x, h, W_irz_words, W_irz_scales, b_irz, W_hrz_words, W_hrz_scales, b_hrz):
    i_rz = ln((mxq(f64(x), 1, "e4m3") @ unpack4(W_irz_words, W_irz_scales)) + f64(b_irz))
    h_rz = ln((mxq(f64(h), 1, "e4m3") @ unpack4(W_hrz_words, W_hrz_scales)) + f64(b_hrz))
    return sigmoid(i_rz + h_rz)

@@ -1,0 +1,260 @@
+from contextlib import ExitStack
+
+import concourse.mybir as mybir
+from concourse.masks import make_identity
+
+F32 = mybir.dt.float32
+BF16 = mybir.dt.bfloat16
+I32 = mybir.dt.int32
+U32 = mybir.dt.uint32
+U8 = mybir.dt.uint8
+FP8X4 = mybir.dt.float8_e4m3fn_x4
+FP4X4 = mybir.dt.float4_e2m1fn_x4
+ALU = mybir.AluOpType
+ACT = mybir.ActivationFunctionType
+
+P = 128
+ROWS = 4096
+K = 512
+PACK = 4
+N = 1024
+BANK = 512
+HALVES = N // BANK
+SIDES = 2
+TILES = 2
+GROUP_ROWS = TILES * P
+N_GROUPS = ROWS // GROUP_ROWS
+EPS = 1e-5
+
+FLOPS = 2 * SIDES * ROWS * K * N
+
+
+def tile_layernormgrucell_pa_t_kernel(
+    tc, x, h, W_irz_words, W_irz_scales, b_irz, W_hrz_words, W_hrz_scales, b_hrz, out
+):
+    nc = tc.nc
+    with ExitStack() as stack:
+        const = stack.enter_context(tc.tile_pool(name="const", bufs=1))
+        rows_pool = stack.enter_context(tc.tile_pool(name="rows", bufs=4))
+        mx_pool = stack.enter_context(tc.tile_pool(name="mx", bufs=2 * TILES))
+        input_pool = stack.enter_context(tc.tile_pool(name="input_side", bufs=3))
+        state_pool = stack.enter_context(tc.tile_pool(name="state_side", bufs=5))
+        scrap_pool = stack.enter_context(tc.tile_pool(name="scrap", bufs=4))
+        stats_pool = stack.enter_context(tc.tile_pool(name="stats", bufs=6))
+        flipped_psum = stack.enter_context(tc.psum_pool(name="flipped", bufs=TILES))
+        product_psum = stack.enter_context(tc.psum_pool(name="product", bufs=6))
+        stack.enter_context(tc.manual_schedule())
+
+        w_planes = const.tile([P, SIDES, N], U8, align_bytes=64)
+        nc.vector.memset(w_planes[:].rearrange("p s n -> p (s n)").bitcast(I32), 0)
+        neg_half = const.tile([P, TILES, SIDES], F32)
+        nc.vector.memset(neg_half[:], -0.5)
+        warm = const.tile([P, 1], F32)
+        nc.vector.memset(warm[:], 0.0)
+        nc.scalar.activation(out=warm[:], in_=warm[:], func=ACT.Sigmoid)
+        ident = const.tile([P, P], F32)
+        make_identity(nc, ident[:])
+
+        w_words = const.tile([P, SIDES, 2 * N], U8, align_bytes=64)
+        bias = const.tile([P, SIDES, N], BF16)
+        given = ((W_irz_words, W_irz_scales, b_irz), (W_hrz_words, W_hrz_scales, b_hrz))
+        for side in range(SIDES):
+            words, scales, b = given[side]
+            nc.sync.dma_start(out=w_words[:, side, :].bitcast(I32), in_=words[0].bitcast(I32))
+            for quadrant in range(4):
+                nc.sync.dma_start(
+                    out=w_planes[32 * quadrant : 32 * quadrant + 4, side, :].bitcast(I32),
+                    in_=scales[0, 4 * quadrant : 4 * quadrant + 4, :].bitcast(I32),
+                )
+            nc.scalar.dma_start(out=bias[:, side, :], in_=b.partition_broadcast(P))
+
+        rows_of = {}
+        flipped_of = {}
+        grouped_of = {}
+        codes_of = {}
+        planes_of = {}
+        input_of = {}
+        state_of = {}
+        sums_of = {}
+        neg_mean_of = {}
+        squares_of = {}
+        rstd_of = {}
+        ratio_of = {}
+        shift_of = {}
+
+        def load(g):
+            rows = rows_pool.tile([P, SIDES, TILES, K], BF16, name="rows")
+            first = g * GROUP_ROWS
+            for side, source in enumerate((x, h)):
+                nc.sync.dma_start(
+                    out=rows[:, side, :, :],
+                    in_=source[first : first + GROUP_ROWS, :].rearrange(
+                        "(p j) k -> p j k", j=TILES
+                    ),
+                )
+            rows_of[g] = rows
+
+        def flip(g):
+            for j in range(TILES):
+                flipped = flipped_psum.tile([P, SIDES, 2, P], F32, name="flipped")
+                for side in range(SIDES):
+                    row_words = rows_of[g][:, side, j, :].bitcast(F32)
+                    for u in range(2):
+                        nc.tensor.transpose(
+                            flipped[:, side, u, :], row_words[:, u : K // 2 : 2], ident[:]
+                        )
+                flipped_of[g, j] = flipped
+
+        def regroup(g):
+            for j in range(TILES):
+                grouped = mx_pool.tile([P, SIDES, P, PACK], BF16, name="grouped", align_bytes=64)
+                nc.scalar.copy(
+                    out=grouped[:].bitcast(F32),
+                    in_=flipped_of[g, j][:].rearrange("p s u r -> p s r u"),
+                )
+                grouped_of[g, j] = grouped
+
+        def quantise(g):
+            for j in range(TILES):
+                codes = mx_pool.tile([P, SIDES, P], U32, name="codes", align_bytes=64)
+                planes = mx_pool.tile([P, SIDES, P], U8, name="planes", align_bytes=64)
+                nc.vector.quantize_mx(
+                    out=codes[:].rearrange("p s r -> p (s r)").bitcast(FP8X4),
+                    scales=planes[:].rearrange("p s r -> p (s r)"),
+                    in_=grouped_of[g, j][:].rearrange("p s r t -> p (s r t)"),
+                )
+                codes_of[g, j] = codes
+                planes_of[g, j] = planes
+
+        def multiply_and_add_bias(g):
+            input_of[g] = input_pool.tile([P, TILES, N], F32, name="input_side")
+            state_of[g] = state_pool.tile([P, TILES, N], F32, name="state_side")
+            sums_of[g] = stats_pool.tile([P, TILES, SIDES, HALVES], F32, name="sums")
+            for j in range(TILES):
+                for side, biased in enumerate((input_of[g], state_of[g])):
+                    for half in range(HALVES):
+                        cols = slice(half * BANK, (half + 1) * BANK)
+                        product = product_psum.tile([P, BANK], F32, name="product")
+                        nc.tensor.matmul_mx(
+                            out=product[:],
+                            lhsT=codes_of[g, j][:, side, :].bitcast(FP8X4),
+                            lhsT_scale=planes_of[g, j][:, side, :],
+                            rhs=w_words[:, side, 2 * half * BANK : 2 * (half + 1) * BANK].bitcast(
+                                FP4X4
+                            ),
+                            rhs_scale=w_planes[:, side, cols],
+                            start=True,
+                            stop=True,
+                        )
+                        nc.vector.scalar_tensor_tensor(
+                            out=biased[:, j, cols],
+                            in0=product[:],
+                            scalar=1.0,
+                            in1=bias[:, side, cols],
+                            op0=ALU.mult,
+                            op1=ALU.add,
+                            accum_out=sums_of[g][:, j, side, half : half + 1],
+                        )
+
+        def mean(g):
+            total = stats_pool.tile([P, TILES, SIDES], F32, name="total")
+            nc.gpsimd.tensor_tensor(
+                out=total[:], in0=sums_of[g][:, :, :, 0], in1=sums_of[g][:, :, :, 1], op=ALU.add
+            )
+            neg_mean = stats_pool.tile([P, TILES, SIDES], F32, name="neg_mean")
+            nc.gpsimd.tensor_scalar(
+                out=neg_mean[:],
+                in0=total[:],
+                scalar1=-1.0 / N,
+                scalar2=0.0,
+                op0=ALU.mult,
+                op1=ALU.add,
+            )
+            neg_mean_of[g] = neg_mean
+
+        def square(g):
+            squares = stats_pool.tile([P, TILES, SIDES], F32, name="squares")
+            for j in range(TILES):
+                for side, biased in enumerate((input_of[g], state_of[g])):
+                    scrap = scrap_pool.tile([P, N], BF16, name="scrap")
+                    nc.scalar.activation(
+                        out=scrap[:],
+                        in_=biased[:, j, :],
+                        func=ACT.Square,
+                        bias=neg_mean_of[g][:, j, side : side + 1],
+                        scale=1.0,
+                        accum_out=squares[:, j, side : side + 1],
+                    )
+            squares_of[g] = squares
+
+        def norm(g):
+            var_eps = stats_pool.tile([P, TILES, SIDES], F32, name="var_eps")
+            nc.gpsimd.tensor_scalar(
+                out=var_eps[:],
+                in0=squares_of[g][:],
+                scalar1=1.0 / N,
+                scalar2=EPS,
+                op0=ALU.mult,
+                op1=ALU.add,
+            )
+            rstd = stats_pool.tile([P, TILES, SIDES], F32, name="rstd")
+            nc.gpsimd.tensor_tensor(out=rstd[:], in0=var_eps[:], in1=neg_half[:], op=ALU.pow)
+            state_std = stats_pool.tile([P, TILES], F32, name="state_std")
+            nc.gpsimd.tensor_tensor(
+                out=state_std[:], in0=var_eps[:, :, 1], in1=rstd[:, :, 1], op=ALU.mult
+            )
+            ratio = stats_pool.tile([P, TILES], F32, name="ratio")
+            nc.gpsimd.tensor_tensor(
+                out=ratio[:], in0=rstd[:, :, 0], in1=state_std[:], op=ALU.mult
+            )
+            shifts = stats_pool.tile([P, TILES, SIDES], F32, name="shifts")
+            nc.gpsimd.tensor_tensor(
+                out=shifts[:], in0=rstd[:], in1=neg_mean_of[g][:], op=ALU.mult
+            )
+            shift = stats_pool.tile([P, TILES], F32, name="shift")
+            nc.gpsimd.tensor_tensor(
+                out=shift[:], in0=shifts[:, :, 0], in1=shifts[:, :, 1], op=ALU.add
+            )
+            rstd_of[g] = rstd
+            ratio_of[g] = ratio
+            shift_of[g] = shift
+
+        def mix(g):
+            for j in range(TILES):
+                nc.vector.scalar_tensor_tensor(
+                    out=state_of[g][:, j, :],
+                    in0=input_of[g][:, j, :],
+                    scalar=ratio_of[g][:, j : j + 1],
+                    in1=state_of[g][:, j, :],
+                    op0=ALU.mult,
+                    op1=ALU.add,
+                )
+
+        def gate_and_store(g):
+            first = g * GROUP_ROWS
+            out_rows = out[first : first + GROUP_ROWS, :].rearrange("(p j) n -> p j n", j=TILES)
+            for j in range(TILES):
+                nc.scalar.activation(
+                    out=state_of[g][:, j, :],
+                    in_=state_of[g][:, j, :],
+                    func=ACT.Sigmoid,
+                    bias=shift_of[g][:, j : j + 1],
+                    scale=rstd_of[g][:, j, 1:2],
+                )
+                nc.sync.dma_start(out=out_rows[:, j, :], in_=state_of[g][:, j, :])
+
+        def run(stage, g):
+            if 0 <= g < N_GROUPS:
+                stage(g)
+
+        for step in range(-4, N_GROUPS + 3):
+            run(load, step + 4)
+            run(regroup, step + 1)
+            run(multiply_and_add_bias, step)
+            run(mean, step)
+            run(quantise, step + 1)
+            run(flip, step + 2)
+            run(gate_and_store, step - 3)
+            run(square, step - 1)
+            run(norm, step - 1)
+            run(mix, step - 2)

@@ -59,14 +59,17 @@ def tile_layernormgrucell_pa_t_kernel(
         bias = const.tile([P, SIDES, N], BF16)
         given = ((W_irz_words, W_irz_scales, b_irz), (W_hrz_words, W_hrz_scales, b_hrz))
         for side in range(SIDES):
-            words, scales, b = given[side]
-            nc.sync.dma_start(out=w_words[:, side, :].bitcast(I32), in_=words[0].bitcast(I32))
-            for quadrant in range(4):
-                nc.sync.dma_start(
-                    out=w_planes[32 * quadrant : 32 * quadrant + 4, side, :].bitcast(I32),
-                    in_=scales[0, 4 * quadrant : 4 * quadrant + 4, :].bitcast(I32),
-                )
-            nc.scalar.dma_start(out=bias[:, side, :], in_=b.partition_broadcast(P))
+            nc.scalar.dma_start(out=bias[:, side, :], in_=given[side][2].partition_broadcast(P))
+
+        def load_weights():
+            for side in range(SIDES):
+                words, scales = given[side][0:2]
+                nc.sync.dma_start(out=w_words[:, side, :].bitcast(I32), in_=words[0].bitcast(I32))
+                for quadrant in range(4):
+                    nc.sync.dma_start(
+                        out=w_planes[32 * quadrant : 32 * quadrant + 4, side, :].bitcast(I32),
+                        in_=scales[0, 4 * quadrant : 4 * quadrant + 4, :].bitcast(I32),
+                    )
 
         rows_of = {}
         flipped_of = {}
@@ -249,6 +252,8 @@ def tile_layernormgrucell_pa_t_kernel(
 
         for step in range(-4, N_GROUPS + 3):
             run(load, step + 4)
+            if step == -4:
+                load_weights()
             run(regroup, step + 1)
             run(multiply_and_add_bias, step)
             run(mean, step)

@@ -45,6 +45,10 @@ def tile_layernormgrucell_pa_t_kernel(
         product_psum = stack.enter_context(tc.psum_pool(name="product", bufs=6))
         stack.enter_context(tc.manual_schedule())
 
+        bias_rows = const.tile([P, SIDES, N], BF16)
+        nc.vector.memset(bias_rows[:], 0.0)
+        ones = const.tile([P, P], BF16)
+        nc.vector.memset(ones[:], 1.0)
         w_planes = const.tile([P, SIDES, N], U8, align_bytes=64)
         nc.vector.memset(w_planes[:].rearrange("p s n -> p (s n)").bitcast(I32), 0)
         neg_half = const.tile([P, TILES, SIDES], F32)
@@ -59,7 +63,19 @@ def tile_layernormgrucell_pa_t_kernel(
         bias = const.tile([P, SIDES, N], BF16)
         given = ((W_irz_words, W_irz_scales, b_irz), (W_hrz_words, W_hrz_scales, b_hrz))
         for side in range(SIDES):
-            nc.scalar.dma_start(out=bias[:, side, :], in_=given[side][2].partition_broadcast(P))
+            nc.scalar.dma_start(
+                out=bias_rows[0:1, side, :], in_=given[side][2].rearrange("(o n) -> o n", o=1)
+            )
+
+        def spread_bias():
+            for side in range(SIDES):
+                for half in range(HALVES):
+                    cols = slice(half * BANK, (half + 1) * BANK)
+                    spread = product_psum.tile([P, BANK], F32, name="product")
+                    nc.tensor.matmul(
+                        out=spread[:], lhsT=ones[:], rhs=bias_rows[:, side, cols], start=True, stop=True
+                    )
+                    nc.scalar.copy(out=bias[:, side, cols], in_=spread[:])
 
         def load_weights():
             for side in range(SIDES):
@@ -258,6 +274,8 @@ def tile_layernormgrucell_pa_t_kernel(
             run(multiply_and_add_bias, step)
             run(mean, step)
             run(quantise, step + 1)
+            if step == -1:
+                spread_bias()
             run(flip, step + 2)
             run(gate_and_store, step - 3)
             run(square, step - 1)

@@ -45,12 +45,12 @@ def tile_layernormgrucell_pa_t_kernel(
         product_psum = stack.enter_context(tc.psum_pool(name="product", bufs=6))
         stack.enter_context(tc.manual_schedule())
 
+        w_planes = const.tile([P, SIDES, N], U8, align_bytes=64)
+        nc.vector.memset(w_planes[:].rearrange("p s n -> p (s n)").bitcast(I32), 0)
         bias_rows = const.tile([P, SIDES, N], BF16)
         nc.vector.memset(bias_rows[:], 0.0)
         ones = const.tile([P, P], BF16)
         nc.vector.memset(ones[:], 1.0)
-        w_planes = const.tile([P, SIDES, N], U8, align_bytes=64)
-        nc.vector.memset(w_planes[:].rearrange("p s n -> p (s n)").bitcast(I32), 0)
         neg_half = const.tile([P, TILES, SIDES], F32)
         nc.vector.memset(neg_half[:], -0.5)
         warm = const.tile([P, 1], F32)
@@ -270,13 +270,18 @@ def tile_layernormgrucell_pa_t_kernel(
             run(load, step + 4)
             if step == -4:
                 load_weights()
-            run(regroup, step + 1)
+            if step != 0:
+                run(regroup, step + 1)
             run(multiply_and_add_bias, step)
             run(mean, step)
+            if step == 0:
+                flip(1)
+                regroup(1)
             run(quantise, step + 1)
             if step == -1:
                 spread_bias()
-            run(flip, step + 2)
+            else:
+                run(flip, step + 2)
             run(gate_and_store, step - 3)
             run(square, step - 1)
             run(norm, step - 1)

@@ -282,7 +282,12 @@ def tile_layernormgrucell_pa_t_kernel(
                 spread_bias()
             else:
                 run(flip, step + 2)
-            run(gate_and_store, step - 3)
-            run(square, step - 1)
-            run(norm, step - 1)
+            if step < N_GROUPS:
+                run(gate_and_store, step - 3)
+                run(square, step - 1)
+                run(norm, step - 1)
+            else:
+                run(square, step - 1)
+                run(norm, step - 1)
+                run(gate_and_store, step - 3)
             run(mix, step - 2)

@@ -25,6 +25,7 @@ TILES = 2
 GROUP_ROWS = TILES * P
 N_GROUPS = ROWS // GROUP_ROWS
 EPS = 1e-5
+WARM_UPS = 3
 
 FLOPS = 2 * SIDES * ROWS * K * N
 
@@ -47,10 +48,15 @@ def tile_layernormgrucell_pa_t_kernel(
 
         w_planes = const.tile([P, SIDES, N], U8, align_bytes=64)
         nc.vector.memset(w_planes[:].rearrange("p s n -> p (s n)").bitcast(I32), 0)
-        bias_rows = const.tile([P, SIDES, N], BF16)
-        nc.vector.memset(bias_rows[:], 0.0)
         ones = const.tile([P, P], BF16)
         nc.vector.memset(ones[:], 1.0)
+        zeros = const.tile([P, BANK], BF16)
+        nc.vector.memset(zeros[:], 0.0)
+        for warm_up in range(WARM_UPS):
+            idle = product_psum.tile([P, BANK], F32, name="product")
+            nc.tensor.matmul(out=idle[:], lhsT=ones[:], rhs=zeros[:], start=True, stop=True)
+        bias_rows = const.tile([P, SIDES, N], BF16)
+        nc.vector.memset(bias_rows[:], 0.0)
         neg_half = const.tile([P, TILES, SIDES], F32)
         nc.vector.memset(neg_half[:], -0.5)
         warm = const.tile([P, 1], F32)

@@ -101,6 +101,7 @@ def tile_layernormgrucell_pa_t_kernel(
         input_of = {}
         state_of = {}
         sums_of = {}
+        total_of = {}
         neg_mean_of = {}
         squares_of = {}
         rstd_of = {}
@@ -151,11 +152,12 @@ def tile_layernormgrucell_pa_t_kernel(
                 codes_of[g, j] = codes
                 planes_of[g, j] = planes
 
-        def multiply_and_add_bias(g):
-            input_of[g] = input_pool.tile([P, TILES, N], F32, name="input_side")
-            state_of[g] = state_pool.tile([P, TILES, N], F32, name="state_side")
-            sums_of[g] = stats_pool.tile([P, TILES, SIDES, HALVES], F32, name="sums")
-            for j in range(TILES):
+        def multiply_and_add_bias(g, j):
+            if j == 0:
+                input_of[g] = input_pool.tile([P, TILES, N], F32, name="input_side")
+                state_of[g] = state_pool.tile([P, TILES, N], F32, name="state_side")
+                sums_of[g] = stats_pool.tile([P, TILES, SIDES, HALVES], F32, name="sums")
+            if True:
                 for side, biased in enumerate((input_of[g], state_of[g])):
                     for half in range(HALVES):
                         cols = slice(half * BANK, (half + 1) * BANK)
@@ -181,11 +183,15 @@ def tile_layernormgrucell_pa_t_kernel(
                             accum_out=sums_of[g][:, j, side, half : half + 1],
                         )
 
-        def mean(g):
+        def add_halves(g):
             total = stats_pool.tile([P, TILES, SIDES], F32, name="total")
             nc.gpsimd.tensor_tensor(
                 out=total[:], in0=sums_of[g][:, :, :, 0], in1=sums_of[g][:, :, :, 1], op=ALU.add
             )
+            total_of[g] = total
+
+        def mean(g):
+            total = total_of[g]
             neg_mean = stats_pool.tile([P, TILES, SIDES], F32, name="neg_mean")
             nc.gpsimd.tensor_scalar(
                 out=neg_mean[:],
@@ -206,8 +212,8 @@ def tile_layernormgrucell_pa_t_kernel(
                         out=scrap[:],
                         in_=biased[:, j, :],
                         func=ACT.Square,
-                        bias=neg_mean_of[g][:, j, side : side + 1],
-                        scale=1.0,
+                        bias=total_of[g][:, j, side : side + 1],
+                        scale=-float(N),
                         accum_out=squares[:, j, side : side + 1],
                     )
             squares_of[g] = squares
@@ -217,7 +223,7 @@ def tile_layernormgrucell_pa_t_kernel(
             nc.gpsimd.tensor_scalar(
                 out=var_eps[:],
                 in0=squares_of[g][:],
-                scalar1=1.0 / N,
+                scalar1=1.0 / N**3,
                 scalar2=EPS,
                 op0=ALU.mult,
                 op1=ALU.add,
@@ -232,16 +238,18 @@ def tile_layernormgrucell_pa_t_kernel(
             nc.gpsimd.tensor_tensor(
                 out=ratio[:], in0=rstd[:, :, 0], in1=state_std[:], op=ALU.mult
             )
+            rstd_of[g] = rstd
+            ratio_of[g] = ratio
+
+        def find_shift(g):
             shifts = stats_pool.tile([P, TILES, SIDES], F32, name="shifts")
             nc.gpsimd.tensor_tensor(
-                out=shifts[:], in0=rstd[:], in1=neg_mean_of[g][:], op=ALU.mult
+                out=shifts[:], in0=rstd_of[g][:], in1=neg_mean_of[g][:], op=ALU.mult
             )
             shift = stats_pool.tile([P, TILES], F32, name="shift")
             nc.gpsimd.tensor_tensor(
                 out=shift[:], in0=shifts[:, :, 0], in1=shifts[:, :, 1], op=ALU.add
             )
-            rstd_of[g] = rstd
-            ratio_of[g] = ratio
             shift_of[g] = shift
 
         def mix(g):
@@ -268,32 +276,41 @@ def tile_layernormgrucell_pa_t_kernel(
                 )
                 nc.sync.dma_start(out=out_rows[:, j, :], in_=state_of[g][:, j, :])
 
-        def run(stage, g):
+        def run(stage, g, *which):
             if 0 <= g < N_GROUPS:
-                stage(g)
+                stage(g, *which)
 
-        for step in range(-4, N_GROUPS + 3):
+        last = N_GROUPS - 1
+        for step in range(-4, N_GROUPS + 2):
             run(load, step + 4)
             if step == -4:
                 load_weights()
-            if step != 0:
-                run(regroup, step + 1)
-            run(multiply_and_add_bias, step)
-            run(mean, step)
+            run(multiply_and_add_bias, step, 0)
             if step == 0:
+                run(multiply_and_add_bias, step, 1)
                 flip(1)
                 regroup(1)
             run(quantise, step + 1)
+            if step == last:
+                run(multiply_and_add_bias, step, 1)
+            run(mix, step - 2)
+            if 0 < step < last:
+                run(multiply_and_add_bias, step, 1)
             if step == -1:
                 spread_bias()
             else:
                 run(flip, step + 2)
-            if step < N_GROUPS:
-                run(gate_and_store, step - 3)
-                run(square, step - 1)
-                run(norm, step - 1)
-            else:
-                run(square, step - 1)
-                run(norm, step - 1)
-                run(gate_and_store, step - 3)
-            run(mix, step - 2)
+            run(square, step - 1)
+            if step != last:
+                if step == last + 1:
+                    run(gate_and_store, step - 3)
+                run(gate_and_store, step - 2)
+            if step != -1:
+                run(regroup, step + 2)
+            if step == last:
+                run(add_halves, step)
+            run(norm, step - 1)
+            if step != last:
+                run(add_halves, step)
+            run(mean, step)
+            run(find_shift, step - 1)

@@ -25,7 +25,7 @@ TILES = 2
 GROUP_ROWS = TILES * P
 N_GROUPS = ROWS // GROUP_ROWS
 EPS = 1e-5
-WARM_UPS = 3
+WARM_UPS = 12
 
 FLOPS = 2 * SIDES * ROWS * K * N
 
@@ -46,25 +46,21 @@ def tile_layernormgrucell_pa_t_kernel(
         product_psum = stack.enter_context(tc.psum_pool(name="product", bufs=6))
         stack.enter_context(tc.manual_schedule())
 
-        w_planes = const.tile([P, SIDES, N], U8, align_bytes=64)
-        nc.vector.memset(w_planes[:].rearrange("p s n -> p (s n)").bitcast(I32), 0)
+        bias_rows = const.tile([P, SIDES, N], BF16)
+        nc.vector.memset(bias_rows[:].rearrange("p s n -> p (s n)").bitcast(I32), 0)
         ones = const.tile([P, P], BF16)
         nc.vector.memset(ones[:], 1.0)
-        zeros = const.tile([P, BANK], BF16)
-        nc.vector.memset(zeros[:], 0.0)
-        for warm_up in range(WARM_UPS):
-            idle = product_psum.tile([P, BANK], F32, name="product")
-            nc.tensor.matmul(out=idle[:], lhsT=ones[:], rhs=zeros[:], start=True, stop=True)
-        bias_rows = const.tile([P, SIDES, N], BF16)
-        nc.vector.memset(bias_rows[:], 0.0)
-        neg_half = const.tile([P, TILES, SIDES], F32)
-        nc.vector.memset(neg_half[:], -0.5)
         warm = const.tile([P, 1], F32)
         nc.vector.memset(warm[:], 0.0)
-        nc.scalar.activation(out=warm[:], in_=warm[:], func=ACT.Sigmoid)
+        w_planes = const.tile([P, SIDES, N], U8, align_bytes=64)
+        nc.vector.memset(w_planes[:].rearrange("p s n -> p (s n)").bitcast(I32), 0)
+        neg_half = const.tile([P, TILES, SIDES], F32)
+        nc.vector.memset(neg_half[:], -0.5)
+        for warm_up in range(WARM_UPS):
+            idle = product_psum.tile([P, BANK], F32, name="product")
+            nc.tensor.matmul(out=idle[:, 0:P], lhsT=ones[:], rhs=ones[:], start=True, stop=True)
         ident = const.tile([P, P], F32)
         make_identity(nc, ident[:])
-
         w_words = const.tile([P, SIDES, 2 * N], U8, align_bytes=64)
         bias = const.tile([P, SIDES, N], BF16)
         given = ((W_irz_words, W_irz_scales, b_irz), (W_hrz_words, W_hrz_scales, b_hrz))
@@ -72,26 +68,34 @@ def tile_layernormgrucell_pa_t_kernel(
             nc.scalar.dma_start(
                 out=bias_rows[0:1, side, :], in_=given[side][2].rearrange("(o n) -> o n", o=1)
             )
+        nc.scalar.activation(out=warm[:], in_=warm[:], func=ACT.Sigmoid)
 
-        def spread_bias():
-            for side in range(SIDES):
-                for half in range(HALVES):
-                    cols = slice(half * BANK, (half + 1) * BANK)
-                    spread = product_psum.tile([P, BANK], F32, name="product")
-                    nc.tensor.matmul(
-                        out=spread[:], lhsT=ones[:], rhs=bias_rows[:, side, cols], start=True, stop=True
-                    )
-                    nc.scalar.copy(out=bias[:, side, cols], in_=spread[:])
+        spread_of = {}
 
-        def load_weights():
-            for side in range(SIDES):
-                words, scales = given[side][0:2]
-                nc.sync.dma_start(out=w_words[:, side, :].bitcast(I32), in_=words[0].bitcast(I32))
-                for quadrant in range(4):
-                    nc.sync.dma_start(
-                        out=w_planes[32 * quadrant : 32 * quadrant + 4, side, :].bitcast(I32),
-                        in_=scales[0, 4 * quadrant : 4 * quadrant + 4, :].bitcast(I32),
-                    )
+        def spread_bias(side):
+            for half in range(HALVES):
+                cols = slice(half * BANK, (half + 1) * BANK)
+                spread = product_psum.tile([P, BANK], F32, name="product")
+                nc.tensor.matmul(
+                    out=spread[:], lhsT=ones[:], rhs=bias_rows[:, side, cols], start=True, stop=True
+                )
+                spread_of[side, half] = spread
+
+        def keep_bias(side, half):
+            cols = slice(half * BANK, (half + 1) * BANK)
+            if side == 0:
+                nc.vector.tensor_copy(out=bias[:, side, cols], in_=spread_of[side, half][:])
+            else:
+                nc.scalar.copy(out=bias[:, side, cols], in_=spread_of[side, half][:])
+
+        def load_weights(side):
+            words, scales = given[side][0:2]
+            nc.sync.dma_start(out=w_words[:, side, :].bitcast(I32), in_=words[0].bitcast(I32))
+            for quadrant in range(4):
+                nc.sync.dma_start(
+                    out=w_planes[32 * quadrant : 32 * quadrant + 4, side, :].bitcast(I32),
+                    in_=scales[0, 4 * quadrant : 4 * quadrant + 4, :].bitcast(I32),
+                )
 
         rows_of = {}
         flipped_of = {}
@@ -100,16 +104,18 @@ def tile_layernormgrucell_pa_t_kernel(
         planes_of = {}
         input_of = {}
         state_of = {}
-        sums_of = {}
-        total_of = {}
-        neg_mean_of = {}
-        squares_of = {}
-        rstd_of = {}
-        ratio_of = {}
-        shift_of = {}
+        stats_of = {}
+        both = range(TILES)
+
+        def stats(name, g):
+            if (name, g) not in stats_of:
+                stat = stats_pool.tile([P, TILES, SIDES], F32, name=name)
+                stats_of[name, g] = stat
+            return stats_of[name, g]
 
         def load(g):
             rows = rows_pool.tile([P, SIDES, TILES, K], BF16, name="rows")
+            rows_of[g] = rows
             first = g * GROUP_ROWS
             for side, source in enumerate((x, h)):
                 nc.sync.dma_start(
@@ -118,10 +124,22 @@ def tile_layernormgrucell_pa_t_kernel(
                         "(p j) k -> p j k", j=TILES
                     ),
                 )
-            rows_of[g] = rows
 
-        def flip(g):
-            for j in range(TILES):
+        def load_tile(g, j):
+            if j == 0:
+                rows = rows_pool.tile([P, SIDES, TILES, K], BF16, name="rows")
+                rows_of[g] = rows
+            first = g * GROUP_ROWS
+            for side, source in enumerate((x, h)):
+                nc.sync.dma_start(
+                    out=rows_of[g][:, side, j, :],
+                    in_=source[first : first + GROUP_ROWS, :].rearrange(
+                        "(p j) k -> p j k", j=TILES
+                    )[:, j, :],
+                )
+
+        def flip(g, tiles=both):
+            for j in tiles:
                 flipped = flipped_psum.tile([P, SIDES, 2, P], F32, name="flipped")
                 for side in range(SIDES):
                     row_words = rows_of[g][:, side, j, :].bitcast(F32)
@@ -131,8 +149,8 @@ def tile_layernormgrucell_pa_t_kernel(
                         )
                 flipped_of[g, j] = flipped
 
-        def regroup(g):
-            for j in range(TILES):
+        def regroup(g, tiles=both):
+            for j in tiles:
                 grouped = mx_pool.tile([P, SIDES, P, PACK], BF16, name="grouped", align_bytes=64)
                 nc.scalar.copy(
                     out=grouped[:].bitcast(F32),
@@ -140,8 +158,8 @@ def tile_layernormgrucell_pa_t_kernel(
                 )
                 grouped_of[g, j] = grouped
 
-        def quantise(g):
-            for j in range(TILES):
+        def quantise(g, tiles=both):
+            for j in tiles:
                 codes = mx_pool.tile([P, SIDES, P], U32, name="codes", align_bytes=64)
                 planes = mx_pool.tile([P, SIDES, P], U8, name="planes", align_bytes=64)
                 nc.vector.quantize_mx(
@@ -152,165 +170,219 @@ def tile_layernormgrucell_pa_t_kernel(
                 codes_of[g, j] = codes
                 planes_of[g, j] = planes
 
-        def multiply_and_add_bias(g, j):
-            if j == 0:
-                input_of[g] = input_pool.tile([P, TILES, N], F32, name="input_side")
-                state_of[g] = state_pool.tile([P, TILES, N], F32, name="state_side")
-                sums_of[g] = stats_pool.tile([P, TILES, SIDES, HALVES], F32, name="sums")
-            if True:
-                for side, biased in enumerate((input_of[g], state_of[g])):
-                    for half in range(HALVES):
-                        cols = slice(half * BANK, (half + 1) * BANK)
-                        product = product_psum.tile([P, BANK], F32, name="product")
-                        nc.tensor.matmul_mx(
-                            out=product[:],
-                            lhsT=codes_of[g, j][:, side, :].bitcast(FP8X4),
-                            lhsT_scale=planes_of[g, j][:, side, :],
-                            rhs=w_words[:, side, 2 * half * BANK : 2 * (half + 1) * BANK].bitcast(
-                                FP4X4
-                            ),
-                            rhs_scale=w_planes[:, side, cols],
-                            start=True,
-                            stop=True,
-                        )
-                        nc.vector.scalar_tensor_tensor(
-                            out=biased[:, j, cols],
-                            in0=product[:],
-                            scalar=1.0,
-                            in1=bias[:, side, cols],
-                            op0=ALU.mult,
-                            op1=ALU.add,
-                            accum_out=sums_of[g][:, j, side, half : half + 1],
-                        )
-
-        def add_halves(g):
-            total = stats_pool.tile([P, TILES, SIDES], F32, name="total")
-            nc.gpsimd.tensor_tensor(
-                out=total[:], in0=sums_of[g][:, :, :, 0], in1=sums_of[g][:, :, :, 1], op=ALU.add
+        def multiply_and_add_bias(g, j, side, half):
+            if (j, side, half) == (0, 0, 0):
+                input_side = input_pool.tile([P, TILES, N], F32, name="input_side")
+                state_side = state_pool.tile([P, TILES, N], F32, name="state_side")
+                sums = stats_pool.tile([P, TILES, SIDES, HALVES], F32, name="sums")
+                input_of[g], state_of[g], stats_of["sums", g] = input_side, state_side, sums
+            cols = slice(half * BANK, (half + 1) * BANK)
+            product = product_psum.tile([P, BANK], F32, name="product")
+            nc.tensor.matmul_mx(
+                out=product[:],
+                lhsT=codes_of[g, j][:, side, :].bitcast(FP8X4),
+                lhsT_scale=planes_of[g, j][:, side, :],
+                rhs=w_words[:, side, 2 * half * BANK : 2 * (half + 1) * BANK].bitcast(FP4X4),
+                rhs_scale=w_planes[:, side, cols],
+                start=True,
+                stop=True,
             )
-            total_of[g] = total
-
-        def mean(g):
-            total = total_of[g]
-            neg_mean = stats_pool.tile([P, TILES, SIDES], F32, name="neg_mean")
-            nc.gpsimd.tensor_scalar(
-                out=neg_mean[:],
-                in0=total[:],
-                scalar1=-1.0 / N,
-                scalar2=0.0,
+            nc.vector.scalar_tensor_tensor(
+                out=(input_of, state_of)[side][g][:, j, cols],
+                in0=product[:],
+                scalar=1.0,
+                in1=bias[:, side, cols],
                 op0=ALU.mult,
                 op1=ALU.add,
+                accum_out=stats_of["sums", g][:, j, side, half : half + 1],
             )
-            neg_mean_of[g] = neg_mean
 
-        def square(g):
-            squares = stats_pool.tile([P, TILES, SIDES], F32, name="squares")
-            for j in range(TILES):
+        def products(g, j, pieces=range(SIDES * HALVES)):
+            for piece in pieces:
+                multiply_and_add_bias(g, j, piece // HALVES, piece % HALVES)
+
+        def add_halves(g, tiles=both):
+            j = slice(tiles[0], tiles[-1] + 1)
+            nc.vector.tensor_reduce(
+                out=stats("total", g)[:, j, :], in_=stats_of["sums", g][:, j, :, :],
+                op=ALU.add, axis=mybir.AxisListType.X,
+            )
+
+        def square(g, tiles=both):
+            for j in tiles:
                 for side, biased in enumerate((input_of[g], state_of[g])):
                     scrap = scrap_pool.tile([P, N], BF16, name="scrap")
                     nc.scalar.activation(
                         out=scrap[:],
                         in_=biased[:, j, :],
                         func=ACT.Square,
-                        bias=total_of[g][:, j, side : side + 1],
+                        bias=stats("total", g)[:, j, side : side + 1],
                         scale=-float(N),
-                        accum_out=squares[:, j, side : side + 1],
+                        accum_out=stats("squares", g)[:, j, side : side + 1],
                     )
-            squares_of[g] = squares
 
-        def norm(g):
-            var_eps = stats_pool.tile([P, TILES, SIDES], F32, name="var_eps")
+        def mean(g):
             nc.gpsimd.tensor_scalar(
-                out=var_eps[:],
-                in0=squares_of[g][:],
-                scalar1=1.0 / N**3,
-                scalar2=EPS,
-                op0=ALU.mult,
-                op1=ALU.add,
+                out=stats("neg_mean", g)[:], in0=stats("total", g)[:],
+                scalar1=-1.0 / N, scalar2=0.0, op0=ALU.mult, op1=ALU.add,
             )
-            rstd = stats_pool.tile([P, TILES, SIDES], F32, name="rstd")
-            nc.gpsimd.tensor_tensor(out=rstd[:], in0=var_eps[:], in1=neg_half[:], op=ALU.pow)
-            state_std = stats_pool.tile([P, TILES], F32, name="state_std")
-            nc.gpsimd.tensor_tensor(
-                out=state_std[:], in0=var_eps[:, :, 1], in1=rstd[:, :, 1], op=ALU.mult
-            )
-            ratio = stats_pool.tile([P, TILES], F32, name="ratio")
-            nc.gpsimd.tensor_tensor(
-                out=ratio[:], in0=rstd[:, :, 0], in1=state_std[:], op=ALU.mult
-            )
-            rstd_of[g] = rstd
-            ratio_of[g] = ratio
 
-        def find_shift(g):
-            shifts = stats_pool.tile([P, TILES, SIDES], F32, name="shifts")
-            nc.gpsimd.tensor_tensor(
-                out=shifts[:], in0=rstd_of[g][:], in1=neg_mean_of[g][:], op=ALU.mult
+        def variance(g, engine, tiles=both):
+            j = slice(tiles[0], tiles[-1] + 1)
+            engine.tensor_scalar(
+                out=stats("var_eps", g)[:, j, :], in0=stats("squares", g)[:, j, :],
+                scalar1=1.0 / N**3, scalar2=EPS, op0=ALU.mult, op1=ALU.add,
             )
-            shift = stats_pool.tile([P, TILES], F32, name="shift")
-            nc.gpsimd.tensor_tensor(
-                out=shift[:], in0=shifts[:, :, 0], in1=shifts[:, :, 1], op=ALU.add
-            )
-            shift_of[g] = shift
 
-        def mix(g):
-            for j in range(TILES):
+        def root(g, tiles=both):
+            j = slice(tiles[0], tiles[-1] + 1)
+            nc.gpsimd.tensor_tensor(
+                out=stats("rstd", g)[:, j, :], in0=stats("var_eps", g)[:, j, :],
+                in1=neg_half[:, j, :], op=ALU.pow,
+            )
+
+        def ratio(g, engine, tiles=both):
+            j = slice(tiles[0], tiles[-1] + 1)
+            engine.tensor_tensor(
+                out=stats("ratio", g)[:, j, 0:1], in0=stats("var_eps", g)[:, j, 1:2],
+                in1=stats("rstd", g)[:, j, 1:2], op=ALU.mult,
+            )
+            engine.tensor_tensor(
+                out=stats("ratio", g)[:, j, 1:2], in0=stats("rstd", g)[:, j, 0:1],
+                in1=stats("ratio", g)[:, j, 0:1], op=ALU.mult,
+            )
+
+        def find_shift(g, engine, tiles=both):
+            j = slice(tiles[0], tiles[-1] + 1)
+            engine.tensor_tensor(
+                out=stats("shifts", g)[:, j, :], in0=stats("rstd", g)[:, j, :],
+                in1=stats("neg_mean", g)[:, j, :], op=ALU.mult,
+            )
+            engine.tensor_tensor(
+                out=stats("shift", g)[:, j, 0:1], in0=stats("shifts", g)[:, j, 0:1],
+                in1=stats("shifts", g)[:, j, 1:2], op=ALU.add,
+            )
+
+        def mix(g, tiles=both):
+            for j in tiles:
                 nc.vector.scalar_tensor_tensor(
                     out=state_of[g][:, j, :],
                     in0=input_of[g][:, j, :],
-                    scalar=ratio_of[g][:, j : j + 1],
+                    scalar=stats("ratio", g)[:, j, 1:2],
                     in1=state_of[g][:, j, :],
                     op0=ALU.mult,
                     op1=ALU.add,
                 )
 
-        def gate_and_store(g):
+        def gate_and_store(g, tiles=both, pieces=1):
             first = g * GROUP_ROWS
             out_rows = out[first : first + GROUP_ROWS, :].rearrange("(p j) n -> p j n", j=TILES)
-            for j in range(TILES):
-                nc.scalar.activation(
-                    out=state_of[g][:, j, :],
-                    in_=state_of[g][:, j, :],
-                    func=ACT.Sigmoid,
-                    bias=shift_of[g][:, j : j + 1],
-                    scale=rstd_of[g][:, j, 1:2],
-                )
-                nc.sync.dma_start(out=out_rows[:, j, :], in_=state_of[g][:, j, :])
+            width = N // pieces
+            for j in tiles:
+                for piece in range(pieces):
+                    cols = slice(piece * width, (piece + 1) * width)
+                    nc.scalar.activation(
+                        out=state_of[g][:, j, cols],
+                        in_=state_of[g][:, j, cols],
+                        func=ACT.Sigmoid,
+                        bias=stats("shift", g)[:, j, 0:1],
+                        scale=stats("rstd", g)[:, j, 1:2],
+                    )
+                    nc.sync.dma_start(out=out_rows[:, j, cols], in_=state_of[g][:, j, cols])
 
-        def run(stage, g, *which):
-            if 0 <= g < N_GROUPS:
-                stage(g, *which)
-
+        load_tile(0, 0)
+        load_weights(0)
+        load_tile(0, 1)
+        load_weights(1)
+        load(1)
+        load(2)
+        load(3)
+        flip(0, [0])
+        spread_bias(0)
+        keep_bias(0, 0)
+        regroup(0, [0])
+        quantise(0, [0])
+        keep_bias(0, 1)
+        flip(0, [1])
+        regroup(0, [1])
+        spread_bias(1)
+        keep_bias(1, 0)
+        keep_bias(1, 1)
+        products(0, 0, [0, 1])
+        quantise(0, [1])
+        products(0, 0, [2, 3])
+        flip(1, [0])
+        regroup(1, [0])
+        products(0, 1, [0])
+        add_halves(0, [0])
+        products(0, 1, [1, 2, 3])
+        flip(1, [1])
+        regroup(1, [1])
+        square(0, [0])
+        quantise(1)
+        flip(2)
+        regroup(2)
+        load(4)
+        products(1, 0, [0])
+        add_halves(0, [1])
+        square(0, [1])
+        products(1, 0, [1, 2, 3])
+        products(1, 1)
+        quantise(2)
+        flip(3)
+        regroup(3)
+        load(5)
+        mean(0)
+        variance(0, nc.gpsimd)
+        root(0)
+        ratio(0, nc.gpsimd)
+        find_shift(0, nc.gpsimd)
         last = N_GROUPS - 1
-        for step in range(-4, N_GROUPS + 2):
-            run(load, step + 4)
-            if step == -4:
-                load_weights()
-            run(multiply_and_add_bias, step, 0)
-            if step == 0:
-                run(multiply_and_add_bias, step, 1)
-                flip(1)
-                regroup(1)
-            run(quantise, step + 1)
-            if step == last:
-                run(multiply_and_add_bias, step, 1)
-            run(mix, step - 2)
-            if 0 < step < last:
-                run(multiply_and_add_bias, step, 1)
-            if step == -1:
-                spread_bias()
-            else:
-                run(flip, step + 2)
-            run(square, step - 1)
-            if step != last:
-                if step == last + 1:
-                    run(gate_and_store, step - 3)
-                run(gate_and_store, step - 2)
-            if step != -1:
-                run(regroup, step + 2)
-            if step == last:
-                run(add_halves, step)
-            run(norm, step - 1)
-            if step != last:
-                run(add_halves, step)
-            run(mean, step)
-            run(find_shift, step - 1)
+        for g in range(2, last):
+            if g + 4 < N_GROUPS:
+                load(g + 4)
+            products(g, 0, [0])
+            add_halves(g - 1)
+            products(g, 0, [1, 2, 3])
+            quantise(g + 1)
+            mix(g - 2)
+            products(g, 1)
+            if g + 2 < N_GROUPS:
+                flip(g + 2)
+            square(g - 1)
+            gate_and_store(g - 2)
+            if g + 2 < N_GROUPS:
+                regroup(g + 2)
+            mean(g - 1)
+            variance(g - 1, nc.gpsimd)
+            root(g - 1)
+            ratio(g - 1, nc.gpsimd)
+            find_shift(g - 1, nc.gpsimd)
+        products(last, 0, [0])
+        add_halves(last - 1)
+        products(last, 0, [1, 2, 3])
+        products(last, 1, [0])
+        add_halves(last, [0])
+        products(last, 1, [1, 2, 3])
+        mean(last - 1)
+        square(last - 1)
+        mix(last - 2, [0])
+        add_halves(last, [1])
+        mix(last - 2, [1])
+        square(last)
+        gate_and_store(last - 2)
+        variance(last - 1, nc.vector)
+        root(last - 1)
+        mean(last)
+        ratio(last - 1, nc.vector)
+        find_shift(last - 1, nc.vector)
+        mix(last - 1)
+        gate_and_store(last - 1)
+        variance(last, nc.vector)
+        root(last)
+        ratio(last, nc.vector)
+        mix(last, [0])
+        find_shift(last, nc.vector)
+        mix(last, [1])
+        gate_and_store(last, [0])
+        gate_and_store(last, [1], 2)

@@ -43,30 +43,33 @@ def tile_layernormgrucell_pa_t_kernel(
         scrap_pool = stack.enter_context(tc.tile_pool(name="scrap", bufs=4))
         stats_pool = stack.enter_context(tc.tile_pool(name="stats", bufs=6))
         flipped_psum = stack.enter_context(tc.psum_pool(name="flipped", bufs=TILES))
-        product_psum = stack.enter_context(tc.psum_pool(name="product", bufs=6))
+        product_psum = stack.enter_context(tc.psum_pool(name="product", bufs=5))
+        mixed_psum = stack.enter_context(tc.psum_pool(name="mixed", bufs=1))
+        diag_pool = stack.enter_context(tc.tile_pool(name="diag", bufs=3))
         stack.enter_context(tc.manual_schedule())
 
-        bias_rows = const.tile([P, SIDES, N], BF16)
-        nc.vector.memset(bias_rows[:].rearrange("p s n -> p (s n)").bitcast(I32), 0)
-        ones = const.tile([P, P], BF16)
-        nc.vector.memset(ones[:], 1.0)
+        bias_rows = const.tile([P, BANK], BF16)
+        nc.vector.memset(bias_rows[:].bitcast(I32), 0)
         warm = const.tile([P, 1], F32)
         nc.vector.memset(warm[:], 0.0)
+        ident = const.tile([P, P], F32)
+        make_identity(nc, ident[:])
+        ident_bf16 = const.tile([P, P], BF16)
+        nc.vector.tensor_copy(out=ident_bf16[:], in_=ident[:])
         w_planes = const.tile([P, SIDES, N], U8, align_bytes=64)
         nc.vector.memset(w_planes[:].rearrange("p s n -> p (s n)").bitcast(I32), 0)
         neg_half = const.tile([P, TILES, SIDES], F32)
         nc.vector.memset(neg_half[:], -0.5)
         for warm_up in range(WARM_UPS):
             idle = product_psum.tile([P, BANK], F32, name="product")
-            nc.tensor.matmul(out=idle[:, 0:P], lhsT=ones[:], rhs=ones[:], start=True, stop=True)
-        ident = const.tile([P, P], F32)
-        make_identity(nc, ident[:])
+            nc.tensor.matmul(out=idle[:, 0:P], lhsT=ident_bf16[:], rhs=ident_bf16[:], start=True, stop=True)
         w_words = const.tile([P, SIDES, 2 * N], U8, align_bytes=64)
         bias = const.tile([P, SIDES, N], BF16)
         given = ((W_irz_words, W_irz_scales, b_irz), (W_hrz_words, W_hrz_scales, b_hrz))
         for side in range(SIDES):
             nc.scalar.dma_start(
-                out=bias_rows[0:1, side, :], in_=given[side][2].rearrange("(o n) -> o n", o=1)
+                out=bias_rows[HALVES * side : HALVES * (side + 1), :],
+                in_=given[side][2].rearrange("(o n) -> o n", o=HALVES),
             )
         nc.scalar.activation(out=warm[:], in_=warm[:], func=ACT.Sigmoid)
 
@@ -74,10 +77,14 @@ def tile_layernormgrucell_pa_t_kernel(
 
         def spread_bias(side):
             for half in range(HALVES):
-                cols = slice(half * BANK, (half + 1) * BANK)
+                row = HALVES * side + half
                 spread = product_psum.tile([P, BANK], F32, name="product")
                 nc.tensor.matmul(
-                    out=spread[:], lhsT=ones[:], rhs=bias_rows[:, side, cols], start=True, stop=True
+                    out=spread[:],
+                    lhsT=ident_bf16[:, row : row + 1].to_broadcast([P, P]),
+                    rhs=bias_rows[:],
+                    start=True,
+                    stop=True,
                 )
                 spread_of[side, half] = spread
 
@@ -149,10 +156,11 @@ def tile_layernormgrucell_pa_t_kernel(
                         )
                 flipped_of[g, j] = flipped
 
-        def regroup(g, tiles=both):
+        def regroup(g, tiles=both, engine=None):
             for j in tiles:
                 grouped = mx_pool.tile([P, SIDES, P, PACK], BF16, name="grouped", align_bytes=64)
-                nc.scalar.copy(
+                copy = nc.scalar.copy if engine is None else nc.vector.tensor_copy
+                copy(
                     out=grouped[:].bitcast(F32),
                     in_=flipped_of[g, j][:].rearrange("p s u r -> p s r u"),
                 )
@@ -265,20 +273,58 @@ def tile_layernormgrucell_pa_t_kernel(
 
         def mix(g, tiles=both):
             for j in tiles:
+                cols = slice(0, BANK if (g, j) in diag_of else N)
                 nc.vector.scalar_tensor_tensor(
-                    out=state_of[g][:, j, :],
-                    in0=input_of[g][:, j, :],
+                    out=state_of[g][:, j, cols],
+                    in0=input_of[g][:, j, cols],
                     scalar=stats("ratio", g)[:, j, 1:2],
-                    in1=state_of[g][:, j, :],
+                    in1=state_of[g][:, j, cols],
                     op0=ALU.mult,
                     op1=ALU.add,
                 )
+
+        diag_of = {}
+        mixed_of = {}
+
+        def prepare_tensor_mix(g, j):
+            diag = diag_pool.tile([P, P], F32, name="diag")
+            nc.gpsimd.tensor_scalar(
+                out=diag[:], in0=ident[:], scalar1=stats("ratio", g)[:, j, 1:2], scalar2=0.0,
+                op0=ALU.mult, op1=ALU.add,
+            )
+            diag_of[g, j] = diag
+
+        def tensor_mix(g, j):
+            cols = slice(BANK, N)
+            mixed = mixed_psum.tile([P, BANK], F32, name="mixed")
+            nc.tensor.matmul(
+                out=mixed[:], lhsT=ident[:], rhs=state_of[g][:, j, cols], start=True, stop=False
+            )
+            nc.tensor.matmul(
+                out=mixed[:], lhsT=diag_of[g, j][:], rhs=input_of[g][:, j, cols],
+                start=False, stop=True,
+            )
+            mixed_of[g, j] = mixed
 
         def gate_and_store(g, tiles=both, pieces=1):
             first = g * GROUP_ROWS
             out_rows = out[first : first + GROUP_ROWS, :].rearrange("(p j) n -> p j n", j=TILES)
             width = N // pieces
             for j in tiles:
+                if (g, j) in mixed_of:
+                    for source, cols in (
+                        (state_of[g][:, j, 0:BANK], slice(0, BANK)),
+                        (mixed_of[g, j][:], slice(BANK, N)),
+                    ):
+                        nc.scalar.activation(
+                            out=state_of[g][:, j, cols],
+                            in_=source,
+                            func=ACT.Sigmoid,
+                            bias=stats("shift", g)[:, j, 0:1],
+                            scale=stats("rstd", g)[:, j, 1:2],
+                        )
+                    nc.sync.dma_start(out=out_rows[:, j, :], in_=state_of[g][:, j, :])
+                    continue
                 for piece in range(pieces):
                     cols = slice(piece * width, (piece + 1) * width)
                     nc.scalar.activation(
@@ -305,19 +351,17 @@ def tile_layernormgrucell_pa_t_kernel(
         keep_bias(0, 1)
         flip(0, [1])
         regroup(0, [1])
+        products(0, 0, [0, 1])
         spread_bias(1)
         keep_bias(1, 0)
         keep_bias(1, 1)
-        products(0, 0, [0, 1])
         quantise(0, [1])
         products(0, 0, [2, 3])
-        flip(1, [0])
-        regroup(1, [0])
+        flip(1)
+        regroup(1)
         products(0, 1, [0])
         add_halves(0, [0])
         products(0, 1, [1, 2, 3])
-        flip(1, [1])
-        regroup(1, [1])
         square(0, [0])
         quantise(1)
         flip(2)
@@ -327,8 +371,10 @@ def tile_layernormgrucell_pa_t_kernel(
         add_halves(0, [1])
         square(0, [1])
         products(1, 0, [1, 2, 3])
+        quantise(2, [0])
         products(1, 1)
-        quantise(2)
+        quantise(2, [1])
+        add_halves(1)
         flip(3)
         regroup(3)
         load(5)
@@ -336,27 +382,35 @@ def tile_layernormgrucell_pa_t_kernel(
         variance(0, nc.gpsimd)
         root(0)
         ratio(0, nc.gpsimd)
+        prepare_tensor_mix(0, 1)
         find_shift(0, nc.gpsimd)
         last = N_GROUPS - 1
         for g in range(2, last):
             if g + 4 < N_GROUPS:
                 load(g + 4)
             products(g, 0, [0])
-            add_halves(g - 1)
+            if g > 2:
+                add_halves(g - 1)
             products(g, 0, [1, 2, 3])
+            if g + 1 > 3 and (g + 1) % 2 == 0:
+                regroup(g + 1, [1], 1)
             quantise(g + 1)
             mix(g - 2)
             products(g, 1)
+            if (g - 2, 1) in diag_of:
+                tensor_mix(g - 2, 1)
             if g + 2 < N_GROUPS:
                 flip(g + 2)
             square(g - 1)
             gate_and_store(g - 2)
             if g + 2 < N_GROUPS:
-                regroup(g + 2)
+                regroup(g + 2, [0] if g + 2 > 3 and (g + 2) % 2 == 0 else both)
             mean(g - 1)
             variance(g - 1, nc.gpsimd)
             root(g - 1)
             ratio(g - 1, nc.gpsimd)
+            if g - 1 < last - 2:
+                prepare_tensor_mix(g - 1, 1)
             find_shift(g - 1, nc.gpsimd)
         products(last, 0, [0])
         add_halves(last - 1)

@@ -48,16 +48,21 @@ def tile_layernormgrucell_pa_t_kernel(
         diag_pool = stack.enter_context(tc.tile_pool(name="diag", bufs=3))
         stack.enter_context(tc.manual_schedule())
 
-        bias_rows = const.tile([P, BANK], BF16)
-        nc.vector.memset(bias_rows[:].bitcast(I32), 0)
+        w_planes = const.tile([P, SIDES, N], U8, align_bytes=64)
+        for side in range(SIDES):
+            nc.vector.memset(w_planes[:, side, :].bitcast(I32), 0)
         warm = const.tile([P, 1], F32)
         nc.vector.memset(warm[:], 0.0)
+        bias_rows = {}
+        for side in range(SIDES):
+            rows_of_bias = const.tile([P, BANK], BF16, name=f"bias_rows_{side}")
+            bias_rows[side] = rows_of_bias
+        nc.gpsimd.memset(bias_rows[0][:].bitcast(I32), 0)
         ident = const.tile([P, P], F32)
         make_identity(nc, ident[:])
+        nc.gpsimd.memset(bias_rows[1][:].bitcast(I32), 0)
         ident_bf16 = const.tile([P, P], BF16)
         nc.vector.tensor_copy(out=ident_bf16[:], in_=ident[:])
-        w_planes = const.tile([P, SIDES, N], U8, align_bytes=64)
-        nc.vector.memset(w_planes[:].rearrange("p s n -> p (s n)").bitcast(I32), 0)
         neg_half = const.tile([P, TILES, SIDES], F32)
         nc.vector.memset(neg_half[:], -0.5)
         for warm_up in range(WARM_UPS):
@@ -66,23 +71,25 @@ def tile_layernormgrucell_pa_t_kernel(
         w_words = const.tile([P, SIDES, 2 * N], U8, align_bytes=64)
         bias = const.tile([P, SIDES, N], BF16)
         given = ((W_irz_words, W_irz_scales, b_irz), (W_hrz_words, W_hrz_scales, b_hrz))
-        for side in range(SIDES):
-            nc.scalar.dma_start(
-                out=bias_rows[HALVES * side : HALVES * (side + 1), :],
+        def load_bias(side):
+            queue = (nc.scalar, nc.sync)[side]
+            queue.dma_start(
+                out=bias_rows[side][0:HALVES, :],
                 in_=given[side][2].rearrange("(o n) -> o n", o=HALVES),
             )
+
+        load_bias(0)
         nc.scalar.activation(out=warm[:], in_=warm[:], func=ACT.Sigmoid)
 
         spread_of = {}
 
         def spread_bias(side):
             for half in range(HALVES):
-                row = HALVES * side + half
                 spread = product_psum.tile([P, BANK], F32, name="product")
                 nc.tensor.matmul(
                     out=spread[:],
-                    lhsT=ident_bf16[:, row : row + 1].to_broadcast([P, P]),
-                    rhs=bias_rows[:],
+                    lhsT=ident_bf16[:, half : half + 1].to_broadcast([P, P]),
+                    rhs=bias_rows[side][:],
                     start=True,
                     stop=True,
                 )
@@ -130,19 +137,6 @@ def tile_layernormgrucell_pa_t_kernel(
                     in_=source[first : first + GROUP_ROWS, :].rearrange(
                         "(p j) k -> p j k", j=TILES
                     ),
-                )
-
-        def load_tile(g, j):
-            if j == 0:
-                rows = rows_pool.tile([P, SIDES, TILES, K], BF16, name="rows")
-                rows_of[g] = rows
-            first = g * GROUP_ROWS
-            for side, source in enumerate((x, h)):
-                nc.sync.dma_start(
-                    out=rows_of[g][:, side, j, :],
-                    in_=source[first : first + GROUP_ROWS, :].rearrange(
-                        "(p j) k -> p j k", j=TILES
-                    )[:, j, :],
                 )
 
         def flip(g, tiles=both):
@@ -336,10 +330,10 @@ def tile_layernormgrucell_pa_t_kernel(
                     )
                     nc.sync.dma_start(out=out_rows[:, j, cols], in_=state_of[g][:, j, cols])
 
-        load_tile(0, 0)
+        load(0)
         load_weights(0)
-        load_tile(0, 1)
         load_weights(1)
+        load_bias(1)
         load(1)
         load(2)
         load(3)

@@ -37,7 +37,7 @@ def tile_layernormgrucell_pa_t_kernel(
     with ExitStack() as stack:
         const = stack.enter_context(tc.tile_pool(name="const", bufs=1))
         rows_pool = stack.enter_context(tc.tile_pool(name="rows", bufs=4))
-        mx_pool = stack.enter_context(tc.tile_pool(name="mx", bufs=2 * TILES))
+        mx_pool = stack.enter_context(tc.tile_pool(name="mx", bufs=3 * TILES))
         input_pool = stack.enter_context(tc.tile_pool(name="input_side", bufs=3))
         state_pool = stack.enter_context(tc.tile_pool(name="state_side", bufs=5))
         scrap_pool = stack.enter_context(tc.tile_pool(name="scrap", bufs=4))
@@ -243,23 +243,29 @@ def tile_layernormgrucell_pa_t_kernel(
                 in1=neg_half[:, j, :], op=ALU.pow,
             )
 
-        def ratio(g, engine, tiles=both):
+        def state_std(g, engine, tiles=both):
             j = slice(tiles[0], tiles[-1] + 1)
             engine.tensor_tensor(
                 out=stats("ratio", g)[:, j, 0:1], in0=stats("var_eps", g)[:, j, 1:2],
                 in1=stats("rstd", g)[:, j, 1:2], op=ALU.mult,
             )
+
+        def ratio(g, engine, tiles=both):
+            j = slice(tiles[0], tiles[-1] + 1)
             engine.tensor_tensor(
                 out=stats("ratio", g)[:, j, 1:2], in0=stats("rstd", g)[:, j, 0:1],
                 in1=stats("ratio", g)[:, j, 0:1], op=ALU.mult,
             )
 
-        def find_shift(g, engine, tiles=both):
+        def find_shifts(g, engine, tiles=both):
             j = slice(tiles[0], tiles[-1] + 1)
             engine.tensor_tensor(
                 out=stats("shifts", g)[:, j, :], in0=stats("rstd", g)[:, j, :],
                 in1=stats("neg_mean", g)[:, j, :], op=ALU.mult,
             )
+
+        def add_shifts(g, engine, tiles=both):
+            j = slice(tiles[0], tiles[-1] + 1)
             engine.tensor_tensor(
                 out=stats("shift", g)[:, j, 0:1], in0=stats("shifts", g)[:, j, 0:1],
                 in1=stats("shifts", g)[:, j, 1:2], op=ALU.add,
@@ -366,18 +372,22 @@ def tile_layernormgrucell_pa_t_kernel(
         square(0, [1])
         products(1, 0, [1, 2, 3])
         quantise(2, [0])
+        load(5)
+        flip(3)
         products(1, 1)
         quantise(2, [1])
         add_halves(1)
-        flip(3)
         regroup(3)
-        load(5)
-        mean(0)
+        flip(4)
+        regroup(4)
         variance(0, nc.gpsimd)
+        mean(0)
         root(0)
+        state_std(0, nc.gpsimd)
+        find_shifts(0, nc.gpsimd)
         ratio(0, nc.gpsimd)
+        add_shifts(0, nc.gpsimd)
         prepare_tensor_mix(0, 1)
-        find_shift(0, nc.gpsimd)
         last = N_GROUPS - 1
         for g in range(2, last):
             if g + 4 < N_GROUPS:
@@ -386,32 +396,35 @@ def tile_layernormgrucell_pa_t_kernel(
             if g > 2:
                 add_halves(g - 1)
             products(g, 0, [1, 2, 3])
-            if g + 1 > 3 and (g + 1) % 2 == 0:
+            if g + 1 > 5 and (g + 1) % 2 == 0:
                 regroup(g + 1, [1], 1)
             quantise(g + 1)
             mix(g - 2)
             products(g, 1)
             if (g - 2, 1) in diag_of:
                 tensor_mix(g - 2, 1)
-            if g + 2 < N_GROUPS:
+            if 4 < g + 2 < N_GROUPS:
                 flip(g + 2)
             square(g - 1)
             gate_and_store(g - 2)
-            if g + 2 < N_GROUPS:
-                regroup(g + 2, [0] if g + 2 > 3 and (g + 2) % 2 == 0 else both)
-            mean(g - 1)
+            if 4 < g + 2 < N_GROUPS:
+                regroup(g + 2, [0] if g + 2 > 5 and (g + 2) % 2 == 0 else both)
             variance(g - 1, nc.gpsimd)
+            mean(g - 1)
             root(g - 1)
+            state_std(g - 1, nc.gpsimd)
+            find_shifts(g - 1, nc.gpsimd)
             ratio(g - 1, nc.gpsimd)
-            if g - 1 < last - 2:
+            add_shifts(g - 1, nc.gpsimd)
+            if g - 1 < last - 1:
                 prepare_tensor_mix(g - 1, 1)
-            find_shift(g - 1, nc.gpsimd)
         products(last, 0, [0])
         add_halves(last - 1)
         products(last, 0, [1, 2, 3])
         products(last, 1, [0])
         add_halves(last, [0])
         products(last, 1, [1, 2, 3])
+        tensor_mix(last - 2, 1)
         mean(last - 1)
         square(last - 1)
         mix(last - 2, [0])
@@ -422,15 +435,18 @@ def tile_layernormgrucell_pa_t_kernel(
         variance(last - 1, nc.vector)
         root(last - 1)
         mean(last)
+        state_std(last - 1, nc.vector)
+        find_shifts(last - 1, nc.vector)
         ratio(last - 1, nc.vector)
-        find_shift(last - 1, nc.vector)
+        add_shifts(last - 1, nc.vector)
         mix(last - 1)
         gate_and_store(last - 1)
         variance(last, nc.vector)
         root(last)
+        state_std(last, nc.vector)
+        find_shifts(last, nc.vector)
         ratio(last, nc.vector)
-        mix(last, [0])
-        find_shift(last, nc.vector)
-        mix(last, [1])
+        add_shifts(last, nc.vector)
+        mix(last)
         gate_and_store(last, [0])
         gate_and_store(last, [1], 2)

@@ -38,8 +38,8 @@ def tile_layernormgrucell_pa_t_kernel(
         const = stack.enter_context(tc.tile_pool(name="const", bufs=1))
         rows_pool = stack.enter_context(tc.tile_pool(name="rows", bufs=4))
         mx_pool = stack.enter_context(tc.tile_pool(name="mx", bufs=3 * TILES))
-        input_pool = stack.enter_context(tc.tile_pool(name="input_side", bufs=3))
-        state_pool = stack.enter_context(tc.tile_pool(name="state_side", bufs=5))
+        input_pool = stack.enter_context(tc.tile_pool(name="input_side", bufs=4))
+        state_pool = stack.enter_context(tc.tile_pool(name="state_side", bufs=6))
         scrap_pool = stack.enter_context(tc.tile_pool(name="scrap", bufs=4))
         stats_pool = stack.enter_context(tc.tile_pool(name="stats", bufs=6))
         flipped_psum = stack.enter_context(tc.psum_pool(name="flipped", bufs=TILES))
@@ -172,12 +172,10 @@ def tile_layernormgrucell_pa_t_kernel(
                 codes_of[g, j] = codes
                 planes_of[g, j] = planes
 
-        def multiply_and_add_bias(g, j, side, half):
-            if (j, side, half) == (0, 0, 0):
-                input_side = input_pool.tile([P, TILES, N], F32, name="input_side")
-                state_side = state_pool.tile([P, TILES, N], F32, name="state_side")
-                sums = stats_pool.tile([P, TILES, SIDES, HALVES], F32, name="sums")
-                input_of[g], state_of[g], stats_of["sums", g] = input_side, state_side, sums
+        product_of = {}
+
+        def multiply(g, j, piece):
+            side, half = piece // HALVES, piece % HALVES
             cols = slice(half * BANK, (half + 1) * BANK)
             product = product_psum.tile([P, BANK], F32, name="product")
             nc.tensor.matmul_mx(
@@ -189,9 +187,19 @@ def tile_layernormgrucell_pa_t_kernel(
                 start=True,
                 stop=True,
             )
+            product_of[g, j, piece] = product
+
+        def add_bias(g, j, piece):
+            side, half = piece // HALVES, piece % HALVES
+            if (j, piece) == (0, 0):
+                input_side = input_pool.tile([P, TILES, N], F32, name="input_side")
+                state_side = state_pool.tile([P, TILES, N], F32, name="state_side")
+                sums = stats_pool.tile([P, TILES, SIDES, HALVES], F32, name="sums")
+                input_of[g], state_of[g], stats_of["sums", g] = input_side, state_side, sums
+            cols = slice(half * BANK, (half + 1) * BANK)
             nc.vector.scalar_tensor_tensor(
                 out=(input_of, state_of)[side][g][:, j, cols],
-                in0=product[:],
+                in0=product_of[g, j, piece][:],
                 scalar=1.0,
                 in1=bias[:, side, cols],
                 op0=ALU.mult,
@@ -201,7 +209,8 @@ def tile_layernormgrucell_pa_t_kernel(
 
         def products(g, j, pieces=range(SIDES * HALVES)):
             for piece in pieces:
-                multiply_and_add_bias(g, j, piece // HALVES, piece % HALVES)
+                multiply(g, j, piece)
+                add_bias(g, j, piece)
 
         def add_halves(g, tiles=both):
             j = slice(tiles[0], tiles[-1] + 1)
@@ -273,7 +282,10 @@ def tile_layernormgrucell_pa_t_kernel(
 
         def mix(g, tiles=both):
             for j in tiles:
-                cols = slice(0, BANK if (g, j) in diag_of else N)
+                width = N - BANK * halves_on_tensor(g, j)
+                if width == 0:
+                    continue
+                cols = slice(0, width)
                 nc.vector.scalar_tensor_tensor(
                     out=state_of[g][:, j, cols],
                     in0=input_of[g][:, j, cols],
@@ -294,8 +306,8 @@ def tile_layernormgrucell_pa_t_kernel(
             )
             diag_of[g, j] = diag
 
-        def tensor_mix(g, j):
-            cols = slice(BANK, N)
+        def tensor_mix(g, j, half):
+            cols = slice(half * BANK, (half + 1) * BANK)
             mixed = mixed_psum.tile([P, BANK], F32, name="mixed")
             nc.tensor.matmul(
                 out=mixed[:], lhsT=ident[:], rhs=state_of[g][:, j, cols], start=True, stop=False
@@ -304,37 +316,38 @@ def tile_layernormgrucell_pa_t_kernel(
                 out=mixed[:], lhsT=diag_of[g, j][:], rhs=input_of[g][:, j, cols],
                 start=False, stop=True,
             )
-            mixed_of[g, j] = mixed
+            mixed_of[g, j, half] = mixed
 
-        def gate_and_store(g, tiles=both, pieces=1):
+        def halves_on_tensor(g, j):
+            if j == 0 or g > last - 2:
+                return 0
+            return 2 if g % 2 == 1 and g < last - 3 else 1
+
+        def gate_and_store(g, j, cols, source=None):
             first = g * GROUP_ROWS
             out_rows = out[first : first + GROUP_ROWS, :].rearrange("(p j) n -> p j n", j=TILES)
-            width = N // pieces
-            for j in tiles:
-                if (g, j) in mixed_of:
-                    for source, cols in (
-                        (state_of[g][:, j, 0:BANK], slice(0, BANK)),
-                        (mixed_of[g, j][:], slice(BANK, N)),
-                    ):
-                        nc.scalar.activation(
-                            out=state_of[g][:, j, cols],
-                            in_=source,
-                            func=ACT.Sigmoid,
-                            bias=stats("shift", g)[:, j, 0:1],
-                            scale=stats("rstd", g)[:, j, 1:2],
-                        )
-                    nc.sync.dma_start(out=out_rows[:, j, :], in_=state_of[g][:, j, :])
-                    continue
-                for piece in range(pieces):
-                    cols = slice(piece * width, (piece + 1) * width)
-                    nc.scalar.activation(
-                        out=state_of[g][:, j, cols],
-                        in_=state_of[g][:, j, cols],
-                        func=ACT.Sigmoid,
-                        bias=stats("shift", g)[:, j, 0:1],
-                        scale=stats("rstd", g)[:, j, 1:2],
-                    )
-                    nc.sync.dma_start(out=out_rows[:, j, cols], in_=state_of[g][:, j, cols])
+            nc.scalar.activation(
+                out=state_of[g][:, j, cols],
+                in_=state_of[g][:, j, cols] if source is None else source[:],
+                func=ACT.Sigmoid,
+                bias=stats("shift", g)[:, j, 0:1],
+                scale=stats("rstd", g)[:, j, 1:2],
+            )
+            nc.sync.dma_start(out=out_rows[:, j, cols], in_=state_of[g][:, j, cols])
+
+        whole = slice(0, N)
+        column_half = (slice(0, BANK), slice(BANK, N))
+        last = N_GROUPS - 1
+
+        def gates(g):
+            gate_and_store(g, 0, whole)
+            on_tensor = halves_on_tensor(g, 1)
+            if on_tensor == 0:
+                gate_and_store(g, 1, whole)
+            if on_tensor == 1:
+                gate_and_store(g, 1, column_half[0])
+            if on_tensor > 0:
+                gate_and_store(g, 1, column_half[1], mixed_of[g, 1, 1])
 
         load(0)
         load_weights(0)
@@ -388,27 +401,37 @@ def tile_layernormgrucell_pa_t_kernel(
         ratio(0, nc.gpsimd)
         add_shifts(0, nc.gpsimd)
         prepare_tensor_mix(0, 1)
-        last = N_GROUPS - 1
+        for piece in range(4):
+            multiply(2, 0, piece)
         for g in range(2, last):
             if g + 4 < N_GROUPS:
                 load(g + 4)
-            products(g, 0, [0])
-            if g > 2:
-                add_halves(g - 1)
-            products(g, 0, [1, 2, 3])
-            if g + 1 > 5 and (g + 1) % 2 == 0:
+            for piece in range(4):
+                multiply(g, 1, piece)
+                add_bias(g, 0, piece)
+                if piece == 0 and g > 2:
+                    add_halves(g - 1)
+            square(g - 1, [0])
+            if g > 2 and halves_on_tensor(g - 3, 1) == 2:
+                gate_and_store(g - 3, 1, column_half[0], mixed_of[g - 3, 1, 0])
+            square(g - 1, [1])
+            if 4 < g + 2 < N_GROUPS:
+                flip(g + 2)
+            tensor_mix(g - 2, 1, 1)
+            if g + 1 > 4 and (g + 1) % 4 != 1 and g + 1 < last:
                 regroup(g + 1, [1], 1)
             quantise(g + 1)
             mix(g - 2)
-            products(g, 1)
-            if (g - 2, 1) in diag_of:
-                tensor_mix(g - 2, 1)
+            multiply(g + 1, 0, 0)
+            for piece in range(4):
+                add_bias(g, 1, piece)
+                if piece < 3:
+                    multiply(g + 1, 0, piece + 1)
+            gates(g - 2)
+            if halves_on_tensor(g - 2, 1) == 2:
+                tensor_mix(g - 2, 1, 0)
             if 4 < g + 2 < N_GROUPS:
-                flip(g + 2)
-            square(g - 1)
-            gate_and_store(g - 2)
-            if 4 < g + 2 < N_GROUPS:
-                regroup(g + 2, [0] if g + 2 > 5 and (g + 2) % 2 == 0 else both)
+                regroup(g + 2, [0] if g + 2 > 4 and (g + 2) % 4 != 1 and g + 2 < last else both)
             variance(g - 1, nc.gpsimd)
             mean(g - 1)
             root(g - 1)
@@ -416,22 +439,28 @@ def tile_layernormgrucell_pa_t_kernel(
             find_shifts(g - 1, nc.gpsimd)
             ratio(g - 1, nc.gpsimd)
             add_shifts(g - 1, nc.gpsimd)
-            if g - 1 < last - 1:
+            if halves_on_tensor(g - 1, 1) > 0:
                 prepare_tensor_mix(g - 1, 1)
-        products(last, 0, [0])
-        add_halves(last - 1)
-        products(last, 0, [1, 2, 3])
-        products(last, 1, [0])
-        add_halves(last, [0])
-        products(last, 1, [1, 2, 3])
-        tensor_mix(last - 2, 1)
+        for piece in range(4):
+            multiply(last, 1, piece)
+            add_bias(last, 0, piece)
+            if piece == 0:
+                add_halves(last - 1)
+        for piece in range(4):
+            add_bias(last, 1, piece)
+            if piece == 0:
+                add_halves(last, [0])
         mean(last - 1)
-        square(last - 1)
+        square(last - 1, [0])
+        if halves_on_tensor(last - 3, 1) == 2:
+            gate_and_store(last - 3, 1, column_half[0], mixed_of[last - 3, 1, 0])
+        square(last - 1, [1])
+        tensor_mix(last - 2, 1, 1)
         mix(last - 2, [0])
         add_halves(last, [1])
         mix(last - 2, [1])
         square(last)
-        gate_and_store(last - 2)
+        gates(last - 2)
         variance(last - 1, nc.vector)
         root(last - 1)
         mean(last)
@@ -440,7 +469,7 @@ def tile_layernormgrucell_pa_t_kernel(
         ratio(last - 1, nc.vector)
         add_shifts(last - 1, nc.vector)
         mix(last - 1)
-        gate_and_store(last - 1)
+        gates(last - 1)
         variance(last, nc.vector)
         root(last)
         state_std(last, nc.vector)
@@ -448,5 +477,6 @@ def tile_layernormgrucell_pa_t_kernel(
         ratio(last, nc.vector)
         add_shifts(last, nc.vector)
         mix(last)
-        gate_and_store(last, [0])
-        gate_and_store(last, [1], 2)
+        gate_and_store(last, 0, whole)
+        gate_and_store(last, 1, column_half[0])
+        gate_and_store(last, 1, column_half[1])

@@ -212,6 +212,12 @@ def tile_layernormgrucell_pa_t_kernel(
                 multiply(g, j, piece)
                 add_bias(g, j, piece)
 
+        def add_halves_on_gpsimd(g):
+            nc.gpsimd.tensor_tensor(
+                out=stats("total", g)[:], in0=stats_of["sums", g][:, :, :, 0],
+                in1=stats_of["sums", g][:, :, :, 1], op=ALU.add,
+            )
+
         def add_halves(g, tiles=both):
             j = slice(tiles[0], tiles[-1] + 1)
             nc.vector.tensor_reduce(
@@ -409,8 +415,6 @@ def tile_layernormgrucell_pa_t_kernel(
             for piece in range(4):
                 multiply(g, 1, piece)
                 add_bias(g, 0, piece)
-                if piece == 0 and g > 2:
-                    add_halves(g - 1)
             square(g - 1, [0])
             if g > 2 and halves_on_tensor(g - 3, 1) == 2:
                 gate_and_store(g - 3, 1, column_half[0], mixed_of[g - 3, 1, 0])
@@ -418,7 +422,7 @@ def tile_layernormgrucell_pa_t_kernel(
             if 4 < g + 2 < N_GROUPS:
                 flip(g + 2)
             tensor_mix(g - 2, 1, 1)
-            if g + 1 > 4 and (g + 1) % 4 != 1 and g + 1 < last:
+            if g + 1 > 4 and (g + 1) % 4 != 1:
                 regroup(g + 1, [1], 1)
             quantise(g + 1)
             mix(g - 2)
@@ -431,10 +435,11 @@ def tile_layernormgrucell_pa_t_kernel(
             if halves_on_tensor(g - 2, 1) == 2:
                 tensor_mix(g - 2, 1, 0)
             if 4 < g + 2 < N_GROUPS:
-                regroup(g + 2, [0] if g + 2 > 4 and (g + 2) % 4 != 1 and g + 2 < last else both)
+                regroup(g + 2, [0] if g + 2 > 4 and (g + 2) % 4 != 1 else both)
             variance(g - 1, nc.gpsimd)
             mean(g - 1)
             root(g - 1)
+            add_halves_on_gpsimd(g)
             state_std(g - 1, nc.gpsimd)
             find_shifts(g - 1, nc.gpsimd)
             ratio(g - 1, nc.gpsimd)
@@ -444,8 +449,6 @@ def tile_layernormgrucell_pa_t_kernel(
         for piece in range(4):
             multiply(last, 1, piece)
             add_bias(last, 0, piece)
-            if piece == 0:
-                add_halves(last - 1)
         for piece in range(4):
             add_bias(last, 1, piece)
             if piece == 0:
@@ -462,21 +465,27 @@ def tile_layernormgrucell_pa_t_kernel(
         square(last)
         gates(last - 2)
         variance(last - 1, nc.vector)
-        root(last - 1)
+        root(last - 1, [0])
+        root(last - 1, [1])
         mean(last)
-        state_std(last - 1, nc.vector)
-        find_shifts(last - 1, nc.vector)
-        ratio(last - 1, nc.vector)
-        add_shifts(last - 1, nc.vector)
-        mix(last - 1)
+        for j in both:
+            state_std(last - 1, nc.vector, [j])
+            find_shifts(last - 1, nc.vector, [j])
+            ratio(last - 1, nc.vector, [j])
+            add_shifts(last - 1, nc.vector, [j])
+            if j == 1:
+                variance(last, nc.vector, [0])
+                root(last, [0])
+            mix(last - 1, [j])
         gates(last - 1)
-        variance(last, nc.vector)
-        root(last)
-        state_std(last, nc.vector)
-        find_shifts(last, nc.vector)
-        ratio(last, nc.vector)
-        add_shifts(last, nc.vector)
-        mix(last)
+        variance(last, nc.vector, [1])
+        root(last, [1])
+        for j in both:
+            state_std(last, nc.vector, [j])
+            find_shifts(last, nc.vector, [j])
+            ratio(last, nc.vector, [j])
+            add_shifts(last, nc.vector, [j])
+            mix(last, [j])
         gate_and_store(last, 0, whole)
         gate_and_store(last, 1, column_half[0])
         gate_and_store(last, 1, column_half[1])

from contextlib import ExitStack

import concourse.mybir as mybir
from concourse.masks import make_identity

F32 = mybir.dt.float32
BF16 = mybir.dt.bfloat16
I32 = mybir.dt.int32
U32 = mybir.dt.uint32
U8 = mybir.dt.uint8
FP8X4 = mybir.dt.float8_e4m3fn_x4
FP4X4 = mybir.dt.float4_e2m1fn_x4
ALU = mybir.AluOpType
ACT = mybir.ActivationFunctionType

P = 128
ROWS = 4096
K = 512
PACK = 4
N = 1024
BANK = 512
HALVES = N // BANK
SIDES = 2
TILES = 2
GROUP_ROWS = TILES * P
N_GROUPS = ROWS // GROUP_ROWS
EPS = 1e-5
WARM_UPS = 12

FLOPS = 2 * SIDES * ROWS * K * N


def tile_layernormgrucell_pa_t_kernel(
    tc, x, h, W_irz_words, W_irz_scales, b_irz, W_hrz_words, W_hrz_scales, b_hrz, out
):
    nc = tc.nc
    with ExitStack() as stack:
        const = stack.enter_context(tc.tile_pool(name="const", bufs=1))
        rows_pool = stack.enter_context(tc.tile_pool(name="rows", bufs=4))
        mx_pool = stack.enter_context(tc.tile_pool(name="mx", bufs=3 * TILES))
        input_pool = stack.enter_context(tc.tile_pool(name="input_side", bufs=4))
        state_pool = stack.enter_context(tc.tile_pool(name="state_side", bufs=6))
        scrap_pool = stack.enter_context(tc.tile_pool(name="scrap", bufs=4))
        stats_pool = stack.enter_context(tc.tile_pool(name="stats", bufs=6))
        flipped_psum = stack.enter_context(tc.psum_pool(name="flipped", bufs=TILES))
        product_psum = stack.enter_context(tc.psum_pool(name="product", bufs=5))
        mixed_psum = stack.enter_context(tc.psum_pool(name="mixed", bufs=1))
        diag_pool = stack.enter_context(tc.tile_pool(name="diag", bufs=3))
        stack.enter_context(tc.manual_schedule())

        w_planes = const.tile([P, SIDES, N], U8, align_bytes=64)
        for side in range(SIDES):
            nc.vector.memset(w_planes[:, side, :].bitcast(I32), 0)
        warm = const.tile([P, 1], F32)
        nc.vector.memset(warm[:], 0.0)
        bias_rows = {}
        for side in range(SIDES):
            rows_of_bias = const.tile([P, BANK], BF16, name=f"bias_rows_{side}")
            bias_rows[side] = rows_of_bias
        nc.gpsimd.memset(bias_rows[0][:].bitcast(I32), 0)
        ident = const.tile([P, P], F32)
        make_identity(nc, ident[:])
        nc.gpsimd.memset(bias_rows[1][:].bitcast(I32), 0)
        ident_bf16 = const.tile([P, P], BF16)
        nc.vector.tensor_copy(out=ident_bf16[:], in_=ident[:])
        neg_half = const.tile([P, TILES, SIDES], F32)
        nc.vector.memset(neg_half[:], -0.5)
        for warm_up in range(WARM_UPS):
            idle = product_psum.tile([P, BANK], F32, name="product")
            nc.tensor.matmul(out=idle[:, 0:P], lhsT=ident_bf16[:], rhs=ident_bf16[:], start=True, stop=True)
        w_words = const.tile([P, SIDES, 2 * N], U8, align_bytes=64)
        bias = const.tile([P, SIDES, N], BF16)
        given = ((W_irz_words, W_irz_scales, b_irz), (W_hrz_words, W_hrz_scales, b_hrz))
        def load_bias(side):
            queue = (nc.scalar, nc.sync)[side]
            queue.dma_start(
                out=bias_rows[side][0:HALVES, :],
                in_=given[side][2].rearrange("(o n) -> o n", o=HALVES),
            )

        load_bias(0)
        nc.scalar.activation(out=warm[:], in_=warm[:], func=ACT.Sigmoid)

        spread_of = {}

        def spread_bias(side):
            for half in range(HALVES):
                spread = product_psum.tile([P, BANK], F32, name="product")
                nc.tensor.matmul(
                    out=spread[:],
                    lhsT=ident_bf16[:, half : half + 1].to_broadcast([P, P]),
                    rhs=bias_rows[side][:],
                    start=True,
                    stop=True,
                )
                spread_of[side, half] = spread

        def keep_bias(side, half):
            cols = slice(half * BANK, (half + 1) * BANK)
            if side == 0:
                nc.vector.tensor_copy(out=bias[:, side, cols], in_=spread_of[side, half][:])
            else:
                nc.scalar.copy(out=bias[:, side, cols], in_=spread_of[side, half][:])

        def load_weights(side):
            words, scales = given[side][0:2]
            nc.sync.dma_start(out=w_words[:, side, :].bitcast(I32), in_=words[0].bitcast(I32))
            for quadrant in range(4):
                nc.sync.dma_start(
                    out=w_planes[32 * quadrant : 32 * quadrant + 4, side, :].bitcast(I32),
                    in_=scales[0, 4 * quadrant : 4 * quadrant + 4, :].bitcast(I32),
                )

        rows_of = {}
        flipped_of = {}
        grouped_of = {}
        codes_of = {}
        planes_of = {}
        input_of = {}
        state_of = {}
        stats_of = {}
        both = range(TILES)

        def stats(name, g):
            if (name, g) not in stats_of:
                stat = stats_pool.tile([P, TILES, SIDES], F32, name=name)
                stats_of[name, g] = stat
            return stats_of[name, g]

        def load(g):
            rows = rows_pool.tile([P, SIDES, TILES, K], BF16, name="rows")
            rows_of[g] = rows
            first = g * GROUP_ROWS
            for side, source in enumerate((x, h)):
                nc.sync.dma_start(
                    out=rows[:, side, :, :],
                    in_=source[first : first + GROUP_ROWS, :].rearrange(
                        "(p j) k -> p j k", j=TILES
                    ),
                )

        def flip(g, tiles=both):
            for j in tiles:
                flipped = flipped_psum.tile([P, SIDES, 2, P], F32, name="flipped")
                for side in range(SIDES):
                    row_words = rows_of[g][:, side, j, :].bitcast(F32)
                    for u in range(2):
                        nc.tensor.transpose(
                            flipped[:, side, u, :], row_words[:, u : K // 2 : 2], ident[:]
                        )
                flipped_of[g, j] = flipped

        def regroup(g, tiles=both, engine=None):
            for j in tiles:
                grouped = mx_pool.tile([P, SIDES, P, PACK], BF16, name="grouped", align_bytes=64)
                copy = nc.scalar.copy if engine is None else nc.vector.tensor_copy
                copy(
                    out=grouped[:].bitcast(F32),
                    in_=flipped_of[g, j][:].rearrange("p s u r -> p s r u"),
                )
                grouped_of[g, j] = grouped

        def quantise(g, tiles=both):
            for j in tiles:
                codes = mx_pool.tile([P, SIDES, P], U32, name="codes", align_bytes=64)
                planes = mx_pool.tile([P, SIDES, P], U8, name="planes", align_bytes=64)
                nc.vector.quantize_mx(
                    out=codes[:].rearrange("p s r -> p (s r)").bitcast(FP8X4),
                    scales=planes[:].rearrange("p s r -> p (s r)"),
                    in_=grouped_of[g, j][:].rearrange("p s r t -> p (s r t)"),
                )
                codes_of[g, j] = codes
                planes_of[g, j] = planes

        product_of = {}

        def multiply(g, j, piece):
            side, half = piece // HALVES, piece % HALVES
            cols = slice(half * BANK, (half + 1) * BANK)
            product = product_psum.tile([P, BANK], F32, name="product")
            nc.tensor.matmul_mx(
                out=product[:],
                lhsT=codes_of[g, j][:, side, :].bitcast(FP8X4),
                lhsT_scale=planes_of[g, j][:, side, :],
                rhs=w_words[:, side, 2 * half * BANK : 2 * (half + 1) * BANK].bitcast(FP4X4),
                rhs_scale=w_planes[:, side, cols],
                start=True,
                stop=True,
            )
            product_of[g, j, piece] = product

        def add_bias(g, j, piece):
            side, half = piece // HALVES, piece % HALVES
            if (j, piece) == (0, 0):
                input_side = input_pool.tile([P, TILES, N], F32, name="input_side")
                state_side = state_pool.tile([P, TILES, N], F32, name="state_side")
                sums = stats_pool.tile([P, TILES, SIDES, HALVES], F32, name="sums")
                input_of[g], state_of[g], stats_of["sums", g] = input_side, state_side, sums
            cols = slice(half * BANK, (half + 1) * BANK)
            nc.vector.scalar_tensor_tensor(
                out=(input_of, state_of)[side][g][:, j, cols],
                in0=product_of[g, j, piece][:],
                scalar=1.0,
                in1=bias[:, side, cols],
                op0=ALU.mult,
                op1=ALU.add,
                accum_out=stats_of["sums", g][:, j, side, half : half + 1],
            )

        def products(g, j, pieces=range(SIDES * HALVES)):
            for piece in pieces:
                multiply(g, j, piece)
                add_bias(g, j, piece)

        def add_halves_on_gpsimd(g):
            nc.gpsimd.tensor_tensor(
                out=stats("total", g)[:], in0=stats_of["sums", g][:, :, :, 0],
                in1=stats_of["sums", g][:, :, :, 1], op=ALU.add,
            )

        def add_halves(g, tiles=both):
            j = slice(tiles[0], tiles[-1] + 1)
            nc.vector.tensor_reduce(
                out=stats("total", g)[:, j, :], in_=stats_of["sums", g][:, j, :, :],
                op=ALU.add, axis=mybir.AxisListType.X,
            )

        def square(g, tiles=both):
            for j in tiles:
                for side, biased in enumerate((input_of[g], state_of[g])):
                    scrap = scrap_pool.tile([P, N], BF16, name="scrap")
                    nc.scalar.activation(
                        out=scrap[:],
                        in_=biased[:, j, :],
                        func=ACT.Square,
                        bias=stats("total", g)[:, j, side : side + 1],
                        scale=-float(N),
                        accum_out=stats("squares", g)[:, j, side : side + 1],
                    )

        def mean(g):
            nc.gpsimd.tensor_scalar(
                out=stats("neg_mean", g)[:], in0=stats("total", g)[:],
                scalar1=-1.0 / N, scalar2=0.0, op0=ALU.mult, op1=ALU.add,
            )

        def variance(g, engine, tiles=both):
            j = slice(tiles[0], tiles[-1] + 1)
            engine.tensor_scalar(
                out=stats("var_eps", g)[:, j, :], in0=stats("squares", g)[:, j, :],
                scalar1=1.0 / N**3, scalar2=EPS, op0=ALU.mult, op1=ALU.add,
            )

        def root(g, tiles=both):
            j = slice(tiles[0], tiles[-1] + 1)
            nc.gpsimd.tensor_tensor(
                out=stats("rstd", g)[:, j, :], in0=stats("var_eps", g)[:, j, :],
                in1=neg_half[:, j, :], op=ALU.pow,
            )

        def state_std(g, engine, tiles=both):
            j = slice(tiles[0], tiles[-1] + 1)
            engine.tensor_tensor(
                out=stats("ratio", g)[:, j, 0:1], in0=stats("var_eps", g)[:, j, 1:2],
                in1=stats("rstd", g)[:, j, 1:2], op=ALU.mult,
            )

        def ratio(g, engine, tiles=both):
            j = slice(tiles[0], tiles[-1] + 1)
            engine.tensor_tensor(
                out=stats("ratio", g)[:, j, 1:2], in0=stats("rstd", g)[:, j, 0:1],
                in1=stats("ratio", g)[:, j, 0:1], op=ALU.mult,
            )

        def find_shifts(g, engine, tiles=both):
            j = slice(tiles[0], tiles[-1] + 1)
            engine.tensor_tensor(
                out=stats("shifts", g)[:, j, :], in0=stats("rstd", g)[:, j, :],
                in1=stats("neg_mean", g)[:, j, :], op=ALU.mult,
            )

        def add_shifts(g, engine, tiles=both):
            j = slice(tiles[0], tiles[-1] + 1)
            engine.tensor_tensor(
                out=stats("shift", g)[:, j, 0:1], in0=stats("shifts", g)[:, j, 0:1],
                in1=stats("shifts", g)[:, j, 1:2], op=ALU.add,
            )

        def mix(g, tiles=both):
            for j in tiles:
                width = N - BANK * halves_on_tensor(g, j)
                if width == 0:
                    continue
                cols = slice(0, width)
                nc.vector.scalar_tensor_tensor(
                    out=state_of[g][:, j, cols],
                    in0=input_of[g][:, j, cols],
                    scalar=stats("ratio", g)[:, j, 1:2],
                    in1=state_of[g][:, j, cols],
                    op0=ALU.mult,
                    op1=ALU.add,
                )

        diag_of = {}
        mixed_of = {}

        def prepare_tensor_mix(g, j):
            diag = diag_pool.tile([P, P], F32, name="diag")
            nc.gpsimd.tensor_scalar(
                out=diag[:], in0=ident[:], scalar1=stats("ratio", g)[:, j, 1:2], scalar2=0.0,
                op0=ALU.mult, op1=ALU.add,
            )
            diag_of[g, j] = diag

        def tensor_mix(g, j, half):
            cols = slice(half * BANK, (half + 1) * BANK)
            mixed = mixed_psum.tile([P, BANK], F32, name="mixed")
            nc.tensor.matmul(
                out=mixed[:], lhsT=ident[:], rhs=state_of[g][:, j, cols], start=True, stop=False
            )
            nc.tensor.matmul(
                out=mixed[:], lhsT=diag_of[g, j][:], rhs=input_of[g][:, j, cols],
                start=False, stop=True,
            )
            mixed_of[g, j, half] = mixed

        def halves_on_tensor(g, j):
            if j == 0 or g > last - 2:
                return 0
            return 2 if g % 2 == 1 and g < last - 3 else 1

        def gate_and_store(g, j, cols, source=None):
            first = g * GROUP_ROWS
            out_rows = out[first : first + GROUP_ROWS, :].rearrange("(p j) n -> p j n", j=TILES)
            nc.scalar.activation(
                out=state_of[g][:, j, cols],
                in_=state_of[g][:, j, cols] if source is None else source[:],
                func=ACT.Sigmoid,
                bias=stats("shift", g)[:, j, 0:1],
                scale=stats("rstd", g)[:, j, 1:2],
            )
            nc.sync.dma_start(out=out_rows[:, j, cols], in_=state_of[g][:, j, cols])

        whole = slice(0, N)
        column_half = (slice(0, BANK), slice(BANK, N))
        last = N_GROUPS - 1

        def gates(g):
            gate_and_store(g, 0, whole)
            on_tensor = halves_on_tensor(g, 1)
            if on_tensor == 0:
                gate_and_store(g, 1, whole)
            if on_tensor == 1:
                gate_and_store(g, 1, column_half[0])
            if on_tensor > 0:
                gate_and_store(g, 1, column_half[1], mixed_of[g, 1, 1])

        load(0)
        load_weights(0)
        load_weights(1)
        load_bias(1)
        load(1)
        load(2)
        load(3)
        flip(0, [0])
        spread_bias(0)
        keep_bias(0, 0)
        regroup(0, [0])
        quantise(0, [0])
        keep_bias(0, 1)
        flip(0, [1])
        regroup(0, [1])
        products(0, 0, [0, 1])
        spread_bias(1)
        keep_bias(1, 0)
        keep_bias(1, 1)
        quantise(0, [1])
        products(0, 0, [2, 3])
        flip(1)
        regroup(1)
        products(0, 1, [0])
        add_halves(0, [0])
        products(0, 1, [1, 2, 3])
        square(0, [0])
        quantise(1)
        flip(2)
        regroup(2)
        load(4)
        products(1, 0, [0])
        add_halves(0, [1])
        square(0, [1])
        products(1, 0, [1, 2, 3])
        quantise(2, [0])
        load(5)
        flip(3)
        products(1, 1)
        quantise(2, [1])
        add_halves(1)
        regroup(3)
        flip(4)
        regroup(4)
        variance(0, nc.gpsimd)
        mean(0)
        root(0)
        state_std(0, nc.gpsimd)
        find_shifts(0, nc.gpsimd)
        ratio(0, nc.gpsimd)
        add_shifts(0, nc.gpsimd)
        prepare_tensor_mix(0, 1)
        for piece in range(4):
            multiply(2, 0, piece)
        for g in range(2, last):
            if g + 4 < N_GROUPS:
                load(g + 4)
            for piece in range(4):
                multiply(g, 1, piece)
                add_bias(g, 0, piece)
            square(g - 1, [0])
            if g > 2 and halves_on_tensor(g - 3, 1) == 2:
                gate_and_store(g - 3, 1, column_half[0], mixed_of[g - 3, 1, 0])
            square(g - 1, [1])
            if 4 < g + 2 < N_GROUPS:
                flip(g + 2)
            tensor_mix(g - 2, 1, 1)
            if g + 1 > 4 and (g + 1) % 4 != 1:
                regroup(g + 1, [1], 1)
            quantise(g + 1)
            mix(g - 2)
            multiply(g + 1, 0, 0)
            for piece in range(4):
                add_bias(g, 1, piece)
                if piece < 3:
                    multiply(g + 1, 0, piece + 1)
            gates(g - 2)
            if halves_on_tensor(g - 2, 1) == 2:
                tensor_mix(g - 2, 1, 0)
            if 4 < g + 2 < N_GROUPS:
                regroup(g + 2, [0] if g + 2 > 4 and (g + 2) % 4 != 1 else both)
            variance(g - 1, nc.gpsimd)
            mean(g - 1)
            root(g - 1)
            add_halves_on_gpsimd(g)
            state_std(g - 1, nc.gpsimd)
            find_shifts(g - 1, nc.gpsimd)
            ratio(g - 1, nc.gpsimd)
            add_shifts(g - 1, nc.gpsimd)
            if halves_on_tensor(g - 1, 1) > 0:
                prepare_tensor_mix(g - 1, 1)
        for piece in range(4):
            multiply(last, 1, piece)
            add_bias(last, 0, piece)
        for piece in range(4):
            add_bias(last, 1, piece)
            if piece == 0:
                add_halves(last, [0])
        mean(last - 1)
        square(last - 1, [0])
        if halves_on_tensor(last - 3, 1) == 2:
            gate_and_store(last - 3, 1, column_half[0], mixed_of[last - 3, 1, 0])
        square(last - 1, [1])
        tensor_mix(last - 2, 1, 1)
        mix(last - 2, [0])
        add_halves(last, [1])
        mix(last - 2, [1])
        square(last)
        gates(last - 2)
        variance(last - 1, nc.vector)
        root(last - 1, [0])
        root(last - 1, [1])
        mean(last)
        for j in both:
            state_std(last - 1, nc.vector, [j])
            find_shifts(last - 1, nc.vector, [j])
            ratio(last - 1, nc.vector, [j])
            add_shifts(last - 1, nc.vector, [j])
            if j == 1:
                variance(last, nc.vector, [0])
                root(last, [0])
            mix(last - 1, [j])
        gates(last - 1)
        variance(last, nc.vector, [1])
        root(last, [1])
        for j in both:
            state_std(last, nc.vector, [j])
            find_shifts(last, nc.vector, [j])
            ratio(last, nc.vector, [j])
            add_shifts(last, nc.vector, [j])
            mix(last, [j])
        gate_and_store(last, 0, whole)
        gate_and_store(last, 1, column_half[0])
        gate_and_store(last, 1, column_half[1])
